import numpy as np
import ml_dtypes


def mxq(x, axis, fmt="e4m3"):
    dtype, down = {"e4m3": (ml_dtypes.float8_e4m3fn, 7), "e5m2": (ml_dtypes.float8_e5m2, 14)}[fmt]
    v = np.moveaxis(np.asarray(x, np.float32).astype(ml_dtypes.bfloat16).astype(np.float64), axis, -1)
    blocks = v.reshape(v.shape[:-1] + (-1, 32))
    amax = np.abs(blocks).max(-1, keepdims=True)
    byte = np.maximum(np.where(amax > 0, np.frexp(amax)[1] - 1 + 127, 0) - down, 1)
    scale = np.exp2(byte - 127.0)
    codes = (blocks / scale).astype(np.float32).astype(dtype).astype(np.float64)
    return np.moveaxis((codes * scale).reshape(v.shape), -1, axis)


WIDE = False


def mx_kscale(k):
    if not WIDE:
        return np.ones(k)
    levels = np.array([10, -10, 5, -5, 0])
    a = np.random.permutation(np.resize(levels, k // 512 * 4)).reshape(k // 512, 4)
    idx = np.arange(k)
    return np.exp2(a[idx // 512, idx % 128 // 32])


BF16 = ml_dtypes.bfloat16


def bf(x):
    return np.asarray(x, np.float32).astype(BF16)


def f64(x):
    return np.asarray(x).astype(np.float64)


E2M1 = np.array([0.0, 0.5, 1.0, 1.5, 2.0, 3.0, 4.0, 6.0, -0.0, -0.5, -1.0, -1.5, -2.0, -3.0, -4.0, -6.0])


def pack_weight(w, fmt):
    k, n = w.shape
    w = f64(bf(w)).reshape(k // 32, 32, n)
    amax = np.abs(w).max(1)
    if fmt == "e4m3":
        byte = np.frexp(amax)[1] - 1 + 127 - 7
    else:
        mant, ex = np.frexp(amax / 6.0)
        byte = np.where(mant > 0.5, ex, ex - 1) + 127
    byte = np.clip(np.where(amax > 0, byte, 1), 1, 254)
    scaled = (w * np.exp2(127.0 - byte)[:, None, :]).reshape(k, n).astype(np.float32)
    by_word = np.ascontiguousarray(scaled.reshape(k // 512, 128, 4, n).transpose(0, 1, 3, 2))
    if fmt == "e4m3":
        words = by_word.astype(ml_dtypes.float8_e4m3fn).view(np.uint8)
    else:
        c = by_word.astype(ml_dtypes.float4_e2m1fn).view(np.uint8) & 0xF
        words = c[..., 0::2] | (c[..., 1::2] << 4)
    return np.ascontiguousarray(words), np.ascontiguousarray(byte.astype(np.uint8).reshape(k // 512, 16, n))


def unpack_weight(words, scales, fmt):
    g, p, n, _ = words.shape
    if fmt == "e4m3":
        vals = np.ascontiguousarray(words).view(ml_dtypes.float8_e4m3fn).astype(np.float64)
    else:
        nib = np.empty((g, p, n, 4), np.uint8)
        nib[..., 0::2] = words & 0xF
        nib[..., 1::2] = words >> 4
        vals = E2M1[nib]
    vals = vals * np.repeat(np.exp2(scales.astype(np.float64) - 127.0), 8, axis=1)[..., None]
    return vals.transpose(0, 1, 3, 2).reshape(g * 512, n)


B, L, S, D, DA, H, MLP = 2, 3, 1024, 512, 1024, 16, 4096
EPS = 1e-5
FMT = "e4m3"


def layer_norm(u, g, b):
    mu = u.mean(-1, keepdims=True)
    var = ((u - mu) ** 2).mean(-1, keepdims=True)
    return (u - mu) / np.sqrt(var + EPS) * g + b


def grn(st, stq, W_words, W_scales, b, g, be):
    w = np.maximum((stq @ unpack_weight(W_words, W_scales, FMT)).reshape(B, L, S, D) + f64(b), 0.0)
    n = layer_norm(st, f64(g), f64(be))
    return (w + n).sum(1)


def setup_inputs():
    s = mx_kscale(D)
    r = np.random.standard_normal
    layer_outputs = bf(r((B, L, S, D)) * s)
    q_words, q_scales = pack_weight(r((D, D)) / np.sqrt(D) / s[:, None], FMT)
    q_b = bf(r(D) * 0.2)
    q_g = bf(1.0 + 0.1 * r(D))
    q_be = bf(r(D) * 0.1)
    k_words, k_scales = pack_weight(r((D, D)) / np.sqrt(D) / s[:, None], FMT)
    k_b = bf(r(D) * 0.2)
    k_g = bf(1.0 + 0.1 * r(D))
    k_be = bf(r(D) * 0.1)
    v_words, v_scales = pack_weight(r((D, D)) / np.sqrt(D) / s[:, None], FMT)
    v_b = bf(r(D) * 0.2)
    v_g = bf(1.0 + 0.1 * r(D))
    v_be = bf(r(D) * 0.1)
    return {"layer_outputs": layer_outputs,
            "grn_q_W_words": q_words, "grn_q_W_scales": q_scales, "grn_q_b": q_b, "grn_q_g": q_g, "grn_q_be": q_be,
            "grn_k_W_words": k_words, "grn_k_W_scales": k_scales, "grn_k_b": k_b, "grn_k_g": k_g, "grn_k_be": k_be,
            "grn_v_W_words": v_words, "grn_v_W_scales": v_scales, "grn_v_b": v_b, "grn_v_g": v_g, "grn_v_be": v_be}


def reference(layer_outputs, grn_q_W_words, grn_q_W_scales, grn_q_b, grn_q_g, grn_q_be, grn_k_W_words, grn_k_W_scales, grn_k_b, grn_k_g, grn_k_be, grn_v_W_words, grn_v_W_scales, grn_v_b, grn_v_g, grn_v_be):
    st = f64(layer_outputs)
    stq = mxq(st.reshape(B * L * S, D), 1, "e4m3")
    q = grn(st, stq, grn_q_W_words, grn_q_W_scales, grn_q_b, grn_q_g, grn_q_be)
    k = grn(st, stq, grn_k_W_words, grn_k_W_scales, grn_k_b, grn_k_g, grn_k_be)
    v = grn(st, stq, grn_v_W_words, grn_v_W_scales, grn_v_b, grn_v_g, grn_v_be)
    return q, k, v

@@ -1,0 +1,303 @@
+from contextlib import ExitStack
+
+import concourse.mybir as mybir
+from concourse.masks import make_identity
+
+F32 = mybir.dt.float32
+BF16 = mybir.dt.bfloat16
+I32 = mybir.dt.int32
+U32 = mybir.dt.uint32
+U8 = mybir.dt.uint8
+FP8X4 = mybir.dt.float8_e4m3fn_x4
+ALU = mybir.AluOpType
+ACT = mybir.ActivationFunctionType
+
+P = 128
+BATCH, LAYERS, SEQ, D = 2, 3, 1024, 512
+EPS = 1e-5
+BLOCKS = D // P
+CHUNK = 512
+TILES = CHUNK // P
+CHUNKS = BATCH * SEQ // CHUNK
+HALF = CHUNK // 2
+HALVES = CHUNK // HALF
+OUTPUTS = 3
+LAG = BLOCKS * OUTPUTS
+
+FLOPS = 2 * BATCH * LAYERS * SEQ * D * D * OUTPUTS
+
+
+def tile_dcadecoderblock_pa_t_kernel(
+    tc,
+    layer_outputs,
+    q_words, q_scales, q_b, q_g, q_be,
+    k_words, k_scales, k_b, k_g, k_be,
+    v_words, v_scales, v_b, v_g, v_be,
+    out_q, out_k, out_v,
+):
+    nc = tc.nc
+    words_in = (q_words, k_words, v_words)
+    scales_in = (q_scales, k_scales, v_scales)
+    vectors_in = ((q_b, q_g, q_be), (k_b, k_g, k_be), (v_b, v_g, v_be))
+    outs = (out_q, out_k, out_v)
+
+    with ExitStack() as stack:
+        stack.enter_context(tc.manual_schedule())
+        consts = stack.enter_context(tc.tile_pool(name="consts", bufs=1))
+        x_pool = stack.enter_context(tc.tile_pool(name="x", bufs=CHUNKS))
+        small = stack.enter_context(tc.tile_pool(name="small", bufs=2))
+        norm_pool = stack.enter_context(tc.tile_pool(name="norm", bufs=2 * TILES))
+        term_pool = stack.enter_context(tc.tile_pool(name="term", bufs=2))
+        quant = stack.enter_context(tc.tile_pool(name="quant", bufs=LAYERS))
+        code_pool = stack.enter_context(tc.tile_pool(name="codes", bufs=2 * LAYERS))
+        ln_pool = stack.enter_context(tc.tile_pool(name="ln", bufs=3))
+        relu_pool = stack.enter_context(tc.tile_pool(name="relu", bufs=LAG + 4))
+        out_pool = stack.enter_context(tc.tile_pool(name="out", bufs=2 * OUTPUTS))
+        prod_psum = stack.enter_context(tc.psum_pool(name="prod", bufs=4))
+        turn_psum = stack.enter_context(tc.psum_pool(name="turn", bufs=3))
+        sums_psum = stack.enter_context(tc.psum_pool(name="sums", bufs=1))
+
+        ident = consts.tile([P, P], F32)
+        make_identity(nc, ident[:])
+        eps = consts.tile([P, 1], F32)
+        nc.vector.memset(eps[:], EPS)
+        warm = consts.tile([P, 1], F32)
+        nc.scalar.activation(out=warm[:], in_=eps[:], func=ACT.Sqrt)
+
+        def token_view(rows):
+            return rows.rearrange("(p i) f -> p i f", i=TILES)
+
+        def chunk_rows(c):
+            per_batch = SEQ // CHUNK
+            return c // per_batch, slice((c % per_batch) * CHUNK, (c % per_batch + 1) * CHUNK)
+
+        def load_x(c):
+            b, rows = chunk_rows(c)
+            x = x_pool.tile([P, LAYERS, TILES, D], BF16, name="x")
+            for l in range(LAYERS):
+                nc.sync.dma_start(out=x[:, l], in_=token_view(layer_outputs[b, l, rows, :]))
+            return x
+
+        xs = [load_x(0)]
+
+        w_codes = consts.tile([P, OUTPUTS, D], U32, align_bytes=64)
+        w_scales = consts.tile([P, OUTPUTS, D], U8, align_bytes=64)
+        nc.vector.memset(w_scales[:].rearrange("p t n -> p (t n)").bitcast(I32), 0)
+        for t in range(OUTPUTS):
+            nc.sync.dma_start(
+                out=w_codes[:, t, :].bitcast(I32),
+                in_=words_in[t][0].rearrange("p n t -> p (n t)").bitcast(I32),
+            )
+            for quadrant in range(4):
+                nc.sync.dma_start(
+                    out=w_scales[32 * quadrant : 32 * quadrant + 4, t, :].bitcast(I32),
+                    in_=scales_in[t][0, 4 * quadrant : 4 * quadrant + 4, :].bitcast(I32),
+                )
+
+        vector_rows = consts.tile([P, P], BF16)
+        nc.vector.memset(vector_rows[:], 0.0)
+        for t in range(OUTPUTS):
+            for v in range(3):
+                first = BLOCKS * (3 * t + v)
+                nc.scalar.dma_start(
+                    out=vector_rows[first : first + BLOCKS, :],
+                    in_=vectors_in[t][v].rearrange("(j m) -> j m", m=P),
+                )
+        for c in range(1, CHUNKS):
+            xs.append(load_x(c))
+
+        six = {}
+        mean_var = {}
+        totals = {}
+        grouped = {}
+        operands = {}
+        turned_x = {}
+        turned_sums = {}
+        relu_sums = {}
+        norm_terms = {}
+        backs = {}
+        results = {}
+
+        def statistics(c, l, i):
+            if (l, i) == (0, 0):
+                six[c] = small.tile([P, LAYERS, TILES, 6], F32, name="six")
+                mean_var[c] = small.tile([P, LAYERS, TILES, 2], F32, name="mean_var")
+            nc.vector.bn_stats(out=six[c][:, l, i, :], in_=xs[c][:, l, i, :])
+            nc.vector.bn_aggr(out=mean_var[c][:, l, i, :], in_=six[c][:, l, i, :])
+
+        def normalised_sums(c):
+            std = small.tile([P, LAYERS, TILES], F32, name="std")
+            nc.scalar.activation(
+                out=std[:], in_=mean_var[c][:, :, :, 1], func=ACT.Sqrt, bias=eps[:], scale=1.0
+            )
+            rstd = small.tile([P, LAYERS, TILES], F32, name="rstd")
+            nc.vector.reciprocal(out=rstd[:], in_=std[:])
+            shift = small.tile([P, LAYERS, TILES], F32, name="shift")
+            nc.vector.scalar_tensor_tensor(
+                out=shift[:], in0=mean_var[c][:, :, :, 0], scalar=-1.0, in1=rstd[:],
+                op0=ALU.mult, op1=ALU.mult,
+            )
+            totals[c] = []
+            for i in range(TILES):
+                total = norm_pool.tile([P, D], F32, name="total")
+                for l in range(LAYERS):
+                    term = total if l == 0 else term_pool.tile([P, D], F32, name="term")
+                    nc.gpsimd.tensor_scalar(
+                        out=term[:], in0=xs[c][:, l, i, :],
+                        scalar1=rstd[:, l, i : i + 1], scalar2=shift[:, l, i : i + 1],
+                        op0=ALU.mult, op1=ALU.add,
+                    )
+                    if l > 0:
+                        nc.gpsimd.tensor_tensor(out=total[:], in0=total[:], in1=term[:], op=ALU.add)
+                totals[c].append(total)
+
+        def turn_x(c, l, half):
+            bank = turn_psum.tile([P, 2, HALF], F32, name="turned_x", tag="turn")
+            for i in range(HALF // P):
+                x_words = xs[c][:, l, half * (HALF // P) + i, :].bitcast(F32)
+                for u in range(2):
+                    nc.tensor.transpose(bank[:, u, i * P : (i + 1) * P], x_words[:, u : D // 2 : 2], ident[:])
+            turned_x[(c, l, half)] = bank
+
+        def take_x(c, l, half):
+            if half == 0:
+                grouped[(c, l)] = quant.tile([P, CHUNK, 4], BF16, name="grouped", align_bytes=64)
+            words = grouped[(c, l)][:].rearrange("p r t -> p (r t)").bitcast(F32).rearrange("p (r u) -> p r u", u=2)
+            nc.scalar.copy(
+                out=words[:, half * HALF : (half + 1) * HALF, :],
+                in_=turned_x[(c, l, half)][:].rearrange("p u r -> p r u"),
+            )
+
+        def quantise(c, l):
+            codes = code_pool.tile([P, CHUNK], U32, name="codes", align_bytes=64)
+            scales = code_pool.tile([P, CHUNK], U8, name="scales", align_bytes=64)
+            nc.vector.quantize_mx(
+                out=codes[:].bitcast(FP8X4), scales=scales[:], in_=grouped[(c, l)][:].rearrange("p r t -> p (r t)")
+            )
+            operands[(c, l)] = (codes, scales)
+
+        def multiply(c, j, t):
+            block = slice(j * P, (j + 1) * P)
+            relu = relu_pool.tile([P, CHUNK], F32, name="relu")
+            for l in range(LAYERS):
+                codes, scales = operands[(c, l)]
+                prod = prod_psum.tile([P, CHUNK], F32, name="prod")
+                nc.tensor.matmul_mx(
+                    out=prod[:],
+                    lhsT=w_codes[:, t, block].bitcast(FP8X4), lhsT_scale=w_scales[:, t, block],
+                    rhs=codes[:].bitcast(FP8X4), rhs_scale=scales[:],
+                    start=True, stop=True,
+                )
+                if l == 0:
+                    nc.scalar.activation(
+                        out=relu[:], in_=prod[:], func=ACT.Relu, bias=bias[:, t, j : j + 1], scale=1.0
+                    )
+                else:
+                    nc.vector.scalar_tensor_tensor(
+                        out=relu[:], in0=prod[:], scalar=neg_bias[:, t, j : j + 1], in1=relu[:],
+                        op0=ALU.max, op1=ALU.add,
+                    )
+            relu_sums[(c, j, t)] = relu
+
+        def turn_sums(c, j):
+            bank = sums_psum.tile([P, CHUNK], F32, name="turned_sums")
+            for i in range(TILES):
+                nc.tensor.transpose(bank[:, i * P : (i + 1) * P], totals[c][i][:, j * P : (j + 1) * P], ident[:])
+            turned_sums[(c, j)] = bank
+
+        def norm_term(c, j, t):
+            ln = ln_pool.tile([P, CHUNK], F32, name="ln")
+            nc.scalar.activation(
+                out=ln[:], in_=turned_sums[(c, j)][:], func=ACT.Identity,
+                scale=gain[:, t, j : j + 1], bias=offset[:, t, j : j + 1],
+            )
+            norm_terms[(c, j, t)] = ln
+
+        def turn_back(c, j, t):
+            bank = turn_psum.tile([P, TILES, P], F32, name="back", tag="turn")
+            for i in range(TILES):
+                tokens = slice(i * P, (i + 1) * P)
+                nc.tensor.matmul(
+                    out=bank[:, i, :], lhsT=relu_sums[(c, j, t)][:, tokens], rhs=ident[:],
+                    is_transpose=True, start=True, stop=False,
+                )
+                nc.tensor.matmul(
+                    out=bank[:, i, :], lhsT=norm_terms[(c, j, t)][:, tokens], rhs=ident[:],
+                    is_transpose=True, start=False, stop=True,
+                )
+            backs[(c, j, t)] = bank
+
+        def take_back(c, j, t, on_vector):
+            if j == 0:
+                results[(c, t)] = out_pool.tile([P, TILES, D], F32, name="result")
+            result = results[(c, t)]
+            if on_vector:
+                nc.vector.tensor_copy(out=result[:, :, j * P : (j + 1) * P], in_=backs[(c, j, t)][:])
+            else:
+                nc.scalar.copy(out=result[:, :, j * P : (j + 1) * P], in_=backs[(c, j, t)][:])
+            if j == BLOCKS - 1:
+                b, rows = chunk_rows(c)
+                nc.sync.dma_start(out=token_view(outs[t][b, rows, :]), in_=result[:])
+
+        for l in range(LAYERS):
+            for half in range(HALVES):
+                turn_x(0, l, half)
+                take_x(0, l, half)
+            for i in range(TILES):
+                statistics(0, l, i)
+            if l == 0:
+                rows_f32 = consts.tile([P, P], F32)
+                nc.vector.tensor_copy(out=rows_f32[:], in_=vector_rows[:])
+                columns_ps = turn_psum.tile([P, P], F32, tag="turn")
+                nc.tensor.transpose(columns_ps[:], rows_f32[:], ident[:])
+            if l == 1:
+                columns = consts.tile([P, OUTPUTS, 3, BLOCKS], F32)
+                nc.vector.tensor_copy(
+                    out=columns[:].rearrange("p t v j -> p (t v j)"),
+                    in_=columns_ps[:, 0 : OUTPUTS * 3 * BLOCKS],
+                )
+                bias = columns[:, :, 0, :]
+                gain = columns[:, :, 1, :]
+                neg_bias = consts.tile([P, OUTPUTS, BLOCKS], F32)
+                nc.vector.tensor_scalar(out=neg_bias[:], in0=bias, scalar1=-1.0, scalar2=None, op0=ALU.mult)
+                offset = consts.tile([P, OUTPUTS, BLOCKS], F32)
+                nc.vector.tensor_scalar(
+                    out=offset[:], in0=columns[:, :, 2, :], scalar1=float(LAYERS), scalar2=None, op0=ALU.mult
+                )
+                nc.vector.scalar_tensor_tensor(
+                    out=offset[:], in0=bias, scalar=float(LAYERS - 1), in1=offset[:], op0=ALU.mult, op1=ALU.add
+                )
+        normalised_sums(0)
+        for l in range(LAYERS):
+            quantise(0, l)
+
+        units = [(c, j, t) for c in range(CHUNKS) for j in range(BLOCKS) for t in range(OUTPUTS)]
+        later = range(1, CHUNKS)
+        x_halves = [(c, l, half) for c in later for l in range(LAYERS) for half in range(HALVES)]
+        x_tiles = [(c, l, i) for c in later for l in range(LAYERS) for i in range(TILES)]
+        per_chunk = BLOCKS * OUTPUTS
+
+        def unit_at(n):
+            return units[n] if 0 <= n < len(units) else None
+
+        for m in range(len(units) + LAG + 3):
+            if unit_at(m):
+                multiply(*units[m])
+            if 0 < m < CHUNKS * per_chunk and m % per_chunk == 0:
+                normalised_sums(m // per_chunk)
+            if unit_at(m - LAG - 1):
+                norm_term(*units[m - LAG - 1])
+            if m % 2 == 1 and m // 2 < len(x_halves):
+                take_x(*x_halves[m // 2])
+                if x_halves[m // 2][2] == HALVES - 1:
+                    quantise(*x_halves[m // 2][0:2])
+            if unit_at(m - LAG - 3):
+                take_back(*units[m - LAG - 3], on_vector=m >= len(x_tiles))
+            if m < len(x_tiles):
+                statistics(*x_tiles[m])
+            if m % 2 == 0 and m // 2 < len(x_halves):
+                turn_x(*x_halves[m // 2])
+            if unit_at(m - LAG - 2):
+                turn_back(*units[m - LAG - 2])
+            if unit_at(m - LAG) and units[m - LAG][2] == 0:
+                turn_sums(*units[m - LAG][0:2])

@@ -123,6 +123,8 @@ def tile_dcadecoderblock_pa_t_kernel(
                 six[c] = small.tile([P, LAYERS, TILES, 6], F32, name="six")
                 mean_var[c] = small.tile([P, LAYERS, TILES, 2], F32, name="mean_var")
             nc.vector.bn_stats(out=six[c][:, l, i, :], in_=xs[c][:, l, i, :])
+
+        def aggregate(c, l, i):
             nc.vector.bn_aggr(out=mean_var[c][:, l, i, :], in_=six[c][:, l, i, :])
 
         def normalised_sums(c):
@@ -176,28 +178,26 @@ def tile_dcadecoderblock_pa_t_kernel(
             )
             operands[(c, l)] = (codes, scales)
 
-        def multiply(c, j, t):
+        def multiply(c, j, t, l):
             block = slice(j * P, (j + 1) * P)
-            relu = relu_pool.tile([P, CHUNK], F32, name="relu")
-            for l in range(LAYERS):
-                codes, scales = operands[(c, l)]
-                prod = prod_psum.tile([P, CHUNK], F32, name="prod")
-                nc.tensor.matmul_mx(
-                    out=prod[:],
-                    lhsT=w_codes[:, t, block].bitcast(FP8X4), lhsT_scale=w_scales[:, t, block],
-                    rhs=codes[:].bitcast(FP8X4), rhs_scale=scales[:],
-                    start=True, stop=True,
+            codes, scales = operands[(c, l)]
+            prod = prod_psum.tile([P, CHUNK], F32, name="prod")
+            nc.tensor.matmul_mx(
+                out=prod[:],
+                lhsT=w_codes[:, t, block].bitcast(FP8X4), lhsT_scale=w_scales[:, t, block],
+                rhs=codes[:].bitcast(FP8X4), rhs_scale=scales[:],
+                start=True, stop=True,
+            )
+            if l == 0:
+                relu_sums[(c, j, t)] = relu_pool.tile([P, CHUNK], F32, name="relu")
+                nc.scalar.activation(
+                    out=relu_sums[(c, j, t)][:], in_=prod[:], func=ACT.Relu, bias=bias[:, t, j : j + 1], scale=1.0
                 )
-                if l == 0:
-                    nc.scalar.activation(
-                        out=relu[:], in_=prod[:], func=ACT.Relu, bias=bias[:, t, j : j + 1], scale=1.0
-                    )
-                else:
-                    nc.vector.scalar_tensor_tensor(
-                        out=relu[:], in0=prod[:], scalar=neg_bias[:, t, j : j + 1], in1=relu[:],
-                        op0=ALU.max, op1=ALU.add,
-                    )
-            relu_sums[(c, j, t)] = relu
+            else:
+                nc.vector.scalar_tensor_tensor(
+                    out=relu_sums[(c, j, t)][:], in0=prod[:], scalar=neg_bias[:, t, j : j + 1],
+                    in1=relu_sums[(c, j, t)][:], op0=ALU.max, op1=ALU.add,
+                )
 
         def turn_sums(c, j):
             bank = sums_psum.tile([P, CHUNK], F32, name="turned_sums")
@@ -245,6 +245,8 @@ def tile_dcadecoderblock_pa_t_kernel(
                 take_x(0, l, half)
             for i in range(TILES):
                 statistics(0, l, i)
+            for i in range(TILES):
+                aggregate(0, l, i)
             if l == 0:
                 rows_f32 = consts.tile([P, P], F32)
                 nc.vector.tensor_copy(out=rows_f32[:], in_=vector_rows[:])
@@ -282,7 +284,14 @@ def tile_dcadecoderblock_pa_t_kernel(
 
         for m in range(len(units) + LAG + 3):
             if unit_at(m):
-                multiply(*units[m])
+                multiply(*units[m], 0)
+                multiply(*units[m], 1)
+            if m < len(x_tiles):
+                statistics(*x_tiles[m])
+            if unit_at(m):
+                multiply(*units[m], 2)
+            if m < len(x_tiles):
+                aggregate(*x_tiles[m])
             if 0 < m < CHUNKS * per_chunk and m % per_chunk == 0:
                 normalised_sums(m // per_chunk)
             if unit_at(m - LAG - 1):
@@ -293,8 +302,6 @@ def tile_dcadecoderblock_pa_t_kernel(
                     quantise(*x_halves[m // 2][0:2])
             if unit_at(m - LAG - 3):
                 take_back(*units[m - LAG - 3], on_vector=m >= len(x_tiles))
-            if m < len(x_tiles):
-                statistics(*x_tiles[m])
             if m % 2 == 0 and m // 2 < len(x_halves):
                 turn_x(*x_halves[m // 2])
             if unit_at(m - LAG - 2):

@@ -42,17 +42,16 @@ def tile_dcadecoderblock_pa_t_kernel(
     outs = (out_q, out_k, out_v)
 
     with ExitStack() as stack:
-        stack.enter_context(tc.manual_schedule())
         consts = stack.enter_context(tc.tile_pool(name="consts", bufs=1))
         x_pool = stack.enter_context(tc.tile_pool(name="x", bufs=CHUNKS))
         small = stack.enter_context(tc.tile_pool(name="small", bufs=2))
         norm_pool = stack.enter_context(tc.tile_pool(name="norm", bufs=2 * TILES))
         term_pool = stack.enter_context(tc.tile_pool(name="term", bufs=2))
-        quant = stack.enter_context(tc.tile_pool(name="quant", bufs=LAYERS))
+        quant = stack.enter_context(tc.tile_pool(name="quant", bufs=2 * LAYERS))
         code_pool = stack.enter_context(tc.tile_pool(name="codes", bufs=2 * LAYERS))
-        ln_pool = stack.enter_context(tc.tile_pool(name="ln", bufs=3))
-        relu_pool = stack.enter_context(tc.tile_pool(name="relu", bufs=LAG + 4))
-        out_pool = stack.enter_context(tc.tile_pool(name="out", bufs=2 * OUTPUTS))
+        ln_pool = stack.enter_context(tc.tile_pool(name="ln", bufs=4))
+        relu_pool = stack.enter_context(tc.tile_pool(name="relu", bufs=LAG + 5))
+        out_pool = stack.enter_context(tc.tile_pool(name="out", bufs=4))
         prod_psum = stack.enter_context(tc.psum_pool(name="prod", bufs=4))
         turn_psum = stack.enter_context(tc.psum_pool(name="turn", bufs=3))
         sums_psum = stack.enter_context(tc.psum_pool(name="sums", bufs=1))
@@ -116,7 +115,6 @@ def tile_dcadecoderblock_pa_t_kernel(
         relu_sums = {}
         norm_terms = {}
         backs = {}
-        results = {}
 
         def statistics(c, l, i):
             if (l, i) == (0, 0):
@@ -213,31 +211,34 @@ def tile_dcadecoderblock_pa_t_kernel(
             )
             norm_terms[(c, j, t)] = ln
 
-        def turn_back(c, j, t):
+        def merge(c, j, t):
+            nc.vector.tensor_tensor(
+                out=relu_sums[(c, j, t)][:], in0=relu_sums[(c, j, t)][:], in1=norm_terms[(c, j, t)][:], op=ALU.add
+            )
+
+        def turn_back(c, j, t, merged):
             bank = turn_psum.tile([P, TILES, P], F32, name="back", tag="turn")
             for i in range(TILES):
                 tokens = slice(i * P, (i + 1) * P)
                 nc.tensor.matmul(
                     out=bank[:, i, :], lhsT=relu_sums[(c, j, t)][:, tokens], rhs=ident[:],
-                    is_transpose=True, start=True, stop=False,
+                    is_transpose=True, start=True, stop=merged,
                 )
-                nc.tensor.matmul(
-                    out=bank[:, i, :], lhsT=norm_terms[(c, j, t)][:, tokens], rhs=ident[:],
-                    is_transpose=True, start=False, stop=True,
-                )
+                if not merged:
+                    nc.tensor.matmul(
+                        out=bank[:, i, :], lhsT=norm_terms[(c, j, t)][:, tokens], rhs=ident[:],
+                        is_transpose=True, start=False, stop=True,
+                    )
             backs[(c, j, t)] = bank
 
         def take_back(c, j, t, on_vector):
-            if j == 0:
-                results[(c, t)] = out_pool.tile([P, TILES, D], F32, name="result")
-            result = results[(c, t)]
+            result = out_pool.tile([P, TILES, P], F32, name="result")
             if on_vector:
-                nc.vector.tensor_copy(out=result[:, :, j * P : (j + 1) * P], in_=backs[(c, j, t)][:])
+                nc.vector.tensor_copy(out=result[:], in_=backs[(c, j, t)][:])
             else:
-                nc.scalar.copy(out=result[:, :, j * P : (j + 1) * P], in_=backs[(c, j, t)][:])
-            if j == BLOCKS - 1:
-                b, rows = chunk_rows(c)
-                nc.sync.dma_start(out=token_view(outs[t][b, rows, :]), in_=result[:])
+                nc.scalar.copy(out=result[:], in_=backs[(c, j, t)][:])
+            b, rows = chunk_rows(c)
+            nc.sync.dma_start(out=token_view(outs[t][b, rows, j * P : (j + 1) * P]), in_=result[:])
 
         for l in range(LAYERS):
             for half in range(HALVES):
@@ -272,22 +273,30 @@ def tile_dcadecoderblock_pa_t_kernel(
         normalised_sums(0)
         for l in range(LAYERS):
             quantise(0, l)
+        for l in range(LAYERS):
+            for half in range(HALVES):
+                turn_x(1, l, half)
+                take_x(1, l, half)
 
         units = [(c, j, t) for c in range(CHUNKS) for j in range(BLOCKS) for t in range(OUTPUTS)]
-        later = range(1, CHUNKS)
-        x_halves = [(c, l, half) for c in later for l in range(LAYERS) for half in range(HALVES)]
-        x_tiles = [(c, l, i) for c in later for l in range(LAYERS) for i in range(TILES)]
+        x_halves = [(c, l, half) for c in range(2, CHUNKS) for l in range(LAYERS) for half in range(HALVES)]
+        x_tiles = [(c, l, i) for c in range(1, CHUNKS) for l in range(LAYERS) for i in range(TILES)]
         per_chunk = BLOCKS * OUTPUTS
 
         def unit_at(n):
             return units[n] if 0 <= n < len(units) else None
 
-        for m in range(len(units) + LAG + 3):
+        def merged(n):
+            return n + LAG + 2 >= len(x_tiles)
+
+        for m in range(len(units) + LAG + 4):
             if unit_at(m):
                 multiply(*units[m], 0)
                 multiply(*units[m], 1)
             if m < len(x_tiles):
                 statistics(*x_tiles[m])
+            if unit_at(m - LAG - 2) and merged(m - LAG - 2):
+                merge(*units[m - LAG - 2])
             if unit_at(m):
                 multiply(*units[m], 2)
             if m < len(x_tiles):
@@ -296,15 +305,15 @@ def tile_dcadecoderblock_pa_t_kernel(
                 normalised_sums(m // per_chunk)
             if unit_at(m - LAG - 1):
                 norm_term(*units[m - LAG - 1])
-            if m % 2 == 1 and m // 2 < len(x_halves):
-                take_x(*x_halves[m // 2])
-                if x_halves[m // 2][2] == HALVES - 1:
-                    quantise(*x_halves[m // 2][0:2])
+            if m < len(x_tiles) and m % TILES == TILES - 1:
+                quantise(*x_tiles[m][0:2])
+            if 0 < m <= len(x_halves):
+                take_x(*x_halves[m - 1])
+            if unit_at(m - LAG - 4):
+                take_back(*units[m - LAG - 4], on_vector=m >= len(units) and m % 2 == 1)
+            if m < len(x_halves):
+                turn_x(*x_halves[m])
             if unit_at(m - LAG - 3):
-                take_back(*units[m - LAG - 3], on_vector=m >= len(x_tiles))
-            if m % 2 == 0 and m // 2 < len(x_halves):
-                turn_x(*x_halves[m // 2])
-            if unit_at(m - LAG - 2):
-                turn_back(*units[m - LAG - 2])
+                turn_back(*units[m - LAG - 3], merged=merged(m - LAG - 3))
             if unit_at(m - LAG) and units[m - LAG][2] == 0:
                 turn_sums(*units[m - LAG][0:2])

@@ -42,6 +42,7 @@ def tile_dcadecoderblock_pa_t_kernel(
     outs = (out_q, out_k, out_v)
 
     with ExitStack() as stack:
+        stack.enter_context(tc.manual_schedule())
         consts = stack.enter_context(tc.tile_pool(name="consts", bufs=1))
         x_pool = stack.enter_context(tc.tile_pool(name="x", bufs=CHUNKS))
         small = stack.enter_context(tc.tile_pool(name="small", bufs=2))

@@ -24,6 +24,18 @@ HALVES = CHUNK // HALF
 OUTPUTS = 3
 LAG = BLOCKS * OUTPUTS
 
+SHIFT = 6
+LT = 4
+PARTS = 24
+PE_EVERY = 99
+ORDER = 1
+PROD = 3
+TURN = 3
+SUMS = 2
+LEAD = 6
+SPREAD = 1
+XR = 1
+XS = -1
 FLOPS = 2 * BATCH * LAYERS * SEQ * D * D * OUTPUTS
 
 
@@ -45,17 +57,16 @@ def tile_dcadecoderblock_pa_t_kernel(
         stack.enter_context(tc.manual_schedule())
         consts = stack.enter_context(tc.tile_pool(name="consts", bufs=1))
         x_pool = stack.enter_context(tc.tile_pool(name="x", bufs=CHUNKS))
-        small = stack.enter_context(tc.tile_pool(name="small", bufs=2))
-        norm_pool = stack.enter_context(tc.tile_pool(name="norm", bufs=2 * TILES))
-        term_pool = stack.enter_context(tc.tile_pool(name="term", bufs=2))
+        small = stack.enter_context(tc.tile_pool(name="small", bufs=3))
+        part_pool = stack.enter_context(tc.tile_pool(name="part", bufs=PARTS))
         quant = stack.enter_context(tc.tile_pool(name="quant", bufs=2 * LAYERS))
-        code_pool = stack.enter_context(tc.tile_pool(name="codes", bufs=2 * LAYERS))
-        ln_pool = stack.enter_context(tc.tile_pool(name="ln", bufs=4))
-        relu_pool = stack.enter_context(tc.tile_pool(name="relu", bufs=LAG + 5))
-        out_pool = stack.enter_context(tc.tile_pool(name="out", bufs=4))
-        prod_psum = stack.enter_context(tc.psum_pool(name="prod", bufs=4))
-        turn_psum = stack.enter_context(tc.psum_pool(name="turn", bufs=3))
-        sums_psum = stack.enter_context(tc.psum_pool(name="sums", bufs=1))
+        code_pool = stack.enter_context(tc.tile_pool(name="codes", bufs=CHUNKS * LAYERS))
+        ln_pool = stack.enter_context(tc.tile_pool(name="ln", bufs=6))
+        relu_pool = stack.enter_context(tc.tile_pool(name="relu", bufs=LEAD + LT + 7))
+        out_pool = stack.enter_context(tc.tile_pool(name="out", bufs=6))
+        prod_psum = stack.enter_context(tc.psum_pool(name="prod", bufs=PROD))
+        turn_psum = stack.enter_context(tc.psum_pool(name="turn", bufs=TURN))
+        sums_psum = stack.enter_context(tc.psum_pool(name="sums", bufs=SUMS))
 
         ident = consts.tile([P, P], F32)
         make_identity(nc, ident[:])
@@ -71,28 +82,31 @@ def tile_dcadecoderblock_pa_t_kernel(
             per_batch = SEQ // CHUNK
             return c // per_batch, slice((c % per_batch) * CHUNK, (c % per_batch + 1) * CHUNK)
 
-        def load_x(c):
+        def load_x(c, layers):
             b, rows = chunk_rows(c)
-            x = x_pool.tile([P, LAYERS, TILES, D], BF16, name="x")
-            for l in range(LAYERS):
-                nc.sync.dma_start(out=x[:, l], in_=token_view(layer_outputs[b, l, rows, :]))
-            return x
+            if len(xs) == c:
+                xs.append(x_pool.tile([P, LAYERS, TILES, D], BF16, name="x"))
+            for l in layers:
+                nc.sync.dma_start(out=xs[c][:, l], in_=token_view(layer_outputs[b, l, rows, :]))
 
-        xs = [load_x(0)]
+        xs = []
+        load_x(0, [0])
 
         w_codes = consts.tile([P, OUTPUTS, D], U32, align_bytes=64)
         w_scales = consts.tile([P, OUTPUTS, D], U8, align_bytes=64)
         nc.vector.memset(w_scales[:].rearrange("p t n -> p (t n)").bitcast(I32), 0)
         for t in range(OUTPUTS):
-            nc.sync.dma_start(
-                out=w_codes[:, t, :].bitcast(I32),
-                in_=words_in[t][0].rearrange("p n t -> p (n t)").bitcast(I32),
-            )
             for quadrant in range(4):
                 nc.sync.dma_start(
                     out=w_scales[32 * quadrant : 32 * quadrant + 4, t, :].bitcast(I32),
                     in_=scales_in[t][0, 4 * quadrant : 4 * quadrant + 4, :].bitcast(I32),
                 )
+        load_x(0, [1, 2])
+        for t in range(OUTPUTS):
+            nc.sync.dma_start(
+                out=w_codes[:, t, :].bitcast(I32),
+                in_=words_in[t][0].rearrange("p n t -> p (n t)").bitcast(I32),
+            )
 
         vector_rows = consts.tile([P, P], BF16)
         nc.vector.memset(vector_rows[:], 0.0)
@@ -104,7 +118,7 @@ def tile_dcadecoderblock_pa_t_kernel(
                     in_=vectors_in[t][v].rearrange("(j m) -> j m", m=P),
                 )
         for c in range(1, CHUNKS):
-            xs.append(load_x(c))
+            load_x(c, range(LAYERS))
 
         six = {}
         mean_var = {}
@@ -126,31 +140,29 @@ def tile_dcadecoderblock_pa_t_kernel(
         def aggregate(c, l, i):
             nc.vector.bn_aggr(out=mean_var[c][:, l, i, :], in_=six[c][:, l, i, :])
 
-        def normalised_sums(c):
-            std = small.tile([P, LAYERS, TILES], F32, name="std")
+        stds = {}
+        rstds = {}
+        parts = {}
+
+        def deviation(c, l):
+            if l == 0:
+                stds[c] = small.tile([P, LAYERS, TILES], F32, name="std")
+                rstds[c] = small.tile([P, LAYERS, TILES], F32, name="rstd")
             nc.scalar.activation(
-                out=std[:], in_=mean_var[c][:, :, :, 1], func=ACT.Sqrt, bias=eps[:], scale=1.0
+                out=stds[c][:, l, :], in_=mean_var[c][:, l, :, 1], func=ACT.Sqrt, bias=eps[:], scale=1.0
             )
-            rstd = small.tile([P, LAYERS, TILES], F32, name="rstd")
-            nc.vector.reciprocal(out=rstd[:], in_=std[:])
-            shift = small.tile([P, LAYERS, TILES], F32, name="shift")
-            nc.vector.scalar_tensor_tensor(
-                out=shift[:], in0=mean_var[c][:, :, :, 0], scalar=-1.0, in1=rstd[:],
-                op0=ALU.mult, op1=ALU.mult,
+
+        def inverse(c, l):
+            nc.vector.reciprocal(out=rstds[c][:, l, :], in_=stds[c][:, l, :])
+
+        def normalise(c, l, i):
+            part = part_pool.tile([P, D], F32, name="part")
+            nc.gpsimd.tensor_scalar(
+                out=part[:], in0=xs[c][:, l, i, :],
+                scalar1=mean_var[c][:, l, i, 0:1], scalar2=rstds[c][:, l, i : i + 1],
+                op0=ALU.subtract, op1=ALU.mult,
             )
-            totals[c] = []
-            for i in range(TILES):
-                total = norm_pool.tile([P, D], F32, name="total")
-                for l in range(LAYERS):
-                    term = total if l == 0 else term_pool.tile([P, D], F32, name="term")
-                    nc.gpsimd.tensor_scalar(
-                        out=term[:], in0=xs[c][:, l, i, :],
-                        scalar1=rstd[:, l, i : i + 1], scalar2=shift[:, l, i : i + 1],
-                        op0=ALU.mult, op1=ALU.add,
-                    )
-                    if l > 0:
-                        nc.gpsimd.tensor_tensor(out=total[:], in0=total[:], in1=term[:], op=ALU.add)
-                totals[c].append(total)
+            parts[(c, l, i)] = part
 
         def turn_x(c, l, half):
             bank = turn_psum.tile([P, 2, HALF], F32, name="turned_x", tag="turn")
@@ -198,11 +210,16 @@ def tile_dcadecoderblock_pa_t_kernel(
                     in1=relu_sums[(c, j, t)][:], op0=ALU.max, op1=ALU.add,
                 )
 
-        def turn_sums(c, j):
-            bank = sums_psum.tile([P, CHUNK], F32, name="turned_sums")
-            for i in range(TILES):
-                nc.tensor.transpose(bank[:, i * P : (i + 1) * P], totals[c][i][:, j * P : (j + 1) * P], ident[:])
-            turned_sums[(c, j)] = bank
+        def turn_sums(c, j, tiles):
+            if tiles[0] == 0:
+                turned_sums[(c, j)] = sums_psum.tile([P, CHUNK], F32, name="turned_sums")
+            bank = turned_sums[(c, j)]
+            for i in tiles:
+                for l in range(LAYERS):
+                    nc.tensor.matmul(
+                        out=bank[:, i * P : (i + 1) * P], lhsT=parts[(c, l, i)][:, j * P : (j + 1) * P], rhs=ident[:],
+                        is_transpose=True, start=l == 0, stop=l == LAYERS - 1,
+                    )
 
         def norm_term(c, j, t):
             ln = ln_pool.tile([P, CHUNK], F32, name="ln")
@@ -212,8 +229,9 @@ def tile_dcadecoderblock_pa_t_kernel(
             )
             norm_terms[(c, j, t)] = ln
 
-        def merge(c, j, t):
-            nc.vector.tensor_tensor(
+        def merge(c, j, t, on_vector):
+            engine = nc.vector if on_vector else nc.gpsimd
+            engine.tensor_tensor(
                 out=relu_sums[(c, j, t)][:], in0=relu_sums[(c, j, t)][:], in1=norm_terms[(c, j, t)][:], op=ALU.add
             )
 
@@ -241,80 +259,108 @@ def tile_dcadecoderblock_pa_t_kernel(
             b, rows = chunk_rows(c)
             nc.sync.dma_start(out=token_view(outs[t][b, rows, j * P : (j + 1) * P]), in_=result[:])
 
+        rows_f32 = consts.tile([P, P], F32)
+        nc.vector.tensor_copy(out=rows_f32[:], in_=vector_rows[:])
+        columns_ps = turn_psum.tile([P, P], F32, tag="turn")
+        nc.tensor.transpose(columns_ps[:], rows_f32[:], ident[:])
+        columns = consts.tile([P, OUTPUTS, 3, BLOCKS], F32)
+        nc.vector.tensor_copy(
+            out=columns[:].rearrange("p t v j -> p (t v j)"),
+            in_=columns_ps[:, 0 : OUTPUTS * 3 * BLOCKS],
+        )
+        bias = columns[:, :, 0, :]
+        gain = columns[:, :, 1, :]
+        neg_bias = consts.tile([P, OUTPUTS, BLOCKS], F32)
+        nc.vector.tensor_scalar(out=neg_bias[:], in0=bias, scalar1=-1.0, scalar2=None, op0=ALU.mult)
+        offset = consts.tile([P, OUTPUTS, BLOCKS], F32)
+        nc.vector.tensor_scalar(
+            out=offset[:], in0=columns[:, :, 2, :], scalar1=float(LAYERS), scalar2=None, op0=ALU.mult
+        )
+        nc.vector.scalar_tensor_tensor(
+            out=offset[:], in0=bias, scalar=float(LAYERS - 1), in1=offset[:], op0=ALU.mult, op1=ALU.add
+        )
         for l in range(LAYERS):
             for half in range(HALVES):
                 turn_x(0, l, half)
                 take_x(0, l, half)
-            for i in range(TILES):
+            for i in range(TILES // 2):
+                statistics(0, l, i)
+            quantise(0, l)
+            for i in range(TILES // 2, TILES):
                 statistics(0, l, i)
             for i in range(TILES):
                 aggregate(0, l, i)
-            if l == 0:
-                rows_f32 = consts.tile([P, P], F32)
-                nc.vector.tensor_copy(out=rows_f32[:], in_=vector_rows[:])
-                columns_ps = turn_psum.tile([P, P], F32, tag="turn")
-                nc.tensor.transpose(columns_ps[:], rows_f32[:], ident[:])
-            if l == 1:
-                columns = consts.tile([P, OUTPUTS, 3, BLOCKS], F32)
-                nc.vector.tensor_copy(
-                    out=columns[:].rearrange("p t v j -> p (t v j)"),
-                    in_=columns_ps[:, 0 : OUTPUTS * 3 * BLOCKS],
-                )
-                bias = columns[:, :, 0, :]
-                gain = columns[:, :, 1, :]
-                neg_bias = consts.tile([P, OUTPUTS, BLOCKS], F32)
-                nc.vector.tensor_scalar(out=neg_bias[:], in0=bias, scalar1=-1.0, scalar2=None, op0=ALU.mult)
-                offset = consts.tile([P, OUTPUTS, BLOCKS], F32)
-                nc.vector.tensor_scalar(
-                    out=offset[:], in0=columns[:, :, 2, :], scalar1=float(LAYERS), scalar2=None, op0=ALU.mult
-                )
-                nc.vector.scalar_tensor_tensor(
-                    out=offset[:], in0=bias, scalar=float(LAYERS - 1), in1=offset[:], op0=ALU.mult, op1=ALU.add
-                )
-        normalised_sums(0)
-        for l in range(LAYERS):
-            quantise(0, l)
-        for l in range(LAYERS):
-            for half in range(HALVES):
-                turn_x(1, l, half)
-                take_x(1, l, half)
+            if l > 0:
+                deviation(0, l - 1)
+                inverse(0, l - 1)
+                for i in range(TILES):
+                    normalise(0, l - 1, i)
 
         units = [(c, j, t) for c in range(CHUNKS) for j in range(BLOCKS) for t in range(OUTPUTS)]
-        x_halves = [(c, l, half) for c in range(2, CHUNKS) for l in range(LAYERS) for half in range(HALVES)]
+        x_halves = [(c, l, half) for c in range(1, CHUNKS) for l in range(LAYERS) for half in range(HALVES)]
         x_tiles = [(c, l, i) for c in range(1, CHUNKS) for l in range(LAYERS) for i in range(TILES)]
-        per_chunk = BLOCKS * OUTPUTS
 
         def unit_at(n):
             return units[n] if 0 <= n < len(units) else None
 
-        def merged(n):
-            return n + LAG + 2 >= len(x_tiles)
+        def tile_at(k):
+            return x_tiles[k] if 0 <= k < len(x_tiles) else None
 
-        for m in range(len(units) + LAG + 4):
+        for m in range(-SHIFT, len(units) + LT + 4):
+            tail = m >= len(units)
+            tile = tile_at(m + SHIFT)
+            if ORDER == 1:
+                if unit_at(m - LT - 3):
+                    take_back(*units[m - LT - 3], on_vector=tail and m % 2 == 1)
+                for h in x_halves[XR * (m - 1 - XS) if m - 1 >= XS else 0 : XR * (m - XS) if m >= XS else 0]:
+                    take_x(*h)
+            if m == -SHIFT + 1:
+                deviation(0, LAYERS - 1)
+            if m == -SHIFT + 2:
+                inverse(0, LAYERS - 1)
+                for i in range(TILES):
+                    normalise(0, LAYERS - 1, i)
             if unit_at(m):
-                multiply(*units[m], 0)
+                if LEAD == 0:
+                    multiply(*units[m], 0)
                 multiply(*units[m], 1)
-            if m < len(x_tiles):
-                statistics(*x_tiles[m])
-            if unit_at(m - LAG - 2) and merged(m - LAG - 2):
-                merge(*units[m - LAG - 2])
+            if tile:
+                statistics(*tile)
+            if unit_at(m - LT - 1) and (tail or (m - LT - 1) % PE_EVERY != 0):
+                merge(*units[m - LT - 1], on_vector=tail)
             if unit_at(m):
                 multiply(*units[m], 2)
-            if m < len(x_tiles):
-                aggregate(*x_tiles[m])
-            if 0 < m < CHUNKS * per_chunk and m % per_chunk == 0:
-                normalised_sums(m // per_chunk)
-            if unit_at(m - LAG - 1):
-                norm_term(*units[m - LAG - 1])
-            if m < len(x_tiles) and m % TILES == TILES - 1:
-                quantise(*x_tiles[m][0:2])
-            if 0 < m <= len(x_halves):
-                take_x(*x_halves[m - 1])
-            if unit_at(m - LAG - 4):
-                take_back(*units[m - LAG - 4], on_vector=m >= len(units) and m % 2 == 1)
-            if m < len(x_halves):
-                turn_x(*x_halves[m])
-            if unit_at(m - LAG - 3):
-                turn_back(*units[m - LAG - 3], merged=merged(m - LAG - 3))
-            if unit_at(m - LAG) and units[m - LAG][2] == 0:
-                turn_sums(*units[m - LAG][0:2])
+            if LEAD > 0 and unit_at(m + LEAD):
+                multiply(*units[m + LEAD], 0)
+            if tile:
+                aggregate(*tile)
+            done = tile_at(m + SHIFT - 1)
+            if done and done[2] == TILES - 1:
+                deviation(*done[0:2])
+            done = tile_at(m + SHIFT - 2)
+            if done and done[2] == TILES - 1:
+                inverse(*done[0:2])
+            if tile_at(m + SHIFT - 6):
+                normalise(*tile_at(m + SHIFT - 6))
+            if unit_at(m - LT):
+                norm_term(*units[m - LT])
+            for k, h in enumerate(x_halves):
+                if h[2] == HALVES - 1 and k // XR + XS + 2 == m:
+                    quantise(*h[0:2])
+            if ORDER == 0:
+                if 0 < m <= len(x_halves):
+                    take_x(*x_halves[m - 1])
+                if unit_at(m - LT - 3):
+                    take_back(*units[m - LT - 3], on_vector=tail and m % 2 == 1)
+            for h in x_halves[XR * (m - XS) if m >= XS else 0 : XR * (m + 1 - XS) if m + 1 >= XS else 0]:
+                turn_x(*h)
+            if unit_at(m - LT - 2):
+                n = m - LT - 2
+                turn_back(*units[n], merged=(n + LT + 1 >= len(units) or n % PE_EVERY != 0))
+            if SPREAD == 0:
+                if unit_at(m - LT + 1) and units[m - LT + 1][2] == 0:
+                    turn_sums(*units[m - LT + 1][0:2], range(TILES))
+            else:
+                for back, tiles in ((3, [0]), (2, [1]), (1, [2, 3])):
+                    if unit_at(m - LT + back) and units[m - LT + back][2] == 0:
+                        turn_sums(*units[m - LT + back][0:2], tiles)

@@ -28,6 +28,7 @@ SHIFT = 6
 LT = 4
 PARTS = 24
 PE_EVERY = 99
+QSHIFT = 0
 ORDER = 1
 PROD = 3
 TURN = 3
@@ -36,6 +37,11 @@ LEAD = 6
 SPREAD = 1
 XR = 1
 XS = -1
+SHIFT_ON = "g"
+RB = 5
+LNB = 4
+OB = 4
+VEXIT = 0
 FLOPS = 2 * BATCH * LAYERS * SEQ * D * D * OUTPUTS
 
 
@@ -61,9 +67,9 @@ def tile_dcadecoderblock_pa_t_kernel(
         part_pool = stack.enter_context(tc.tile_pool(name="part", bufs=PARTS))
         quant = stack.enter_context(tc.tile_pool(name="quant", bufs=2 * LAYERS))
         code_pool = stack.enter_context(tc.tile_pool(name="codes", bufs=CHUNKS * LAYERS))
-        ln_pool = stack.enter_context(tc.tile_pool(name="ln", bufs=6))
-        relu_pool = stack.enter_context(tc.tile_pool(name="relu", bufs=LEAD + LT + 7))
-        out_pool = stack.enter_context(tc.tile_pool(name="out", bufs=6))
+        ln_pool = stack.enter_context(tc.tile_pool(name="ln", bufs=LNB))
+        relu_pool = stack.enter_context(tc.tile_pool(name="relu", bufs=LEAD + LT + RB))
+        out_pool = stack.enter_context(tc.tile_pool(name="out", bufs=OB))
         prod_psum = stack.enter_context(tc.psum_pool(name="prod", bufs=PROD))
         turn_psum = stack.enter_context(tc.psum_pool(name="turn", bufs=TURN))
         sums_psum = stack.enter_context(tc.psum_pool(name="sums", bufs=SUMS))
@@ -91,6 +97,15 @@ def tile_dcadecoderblock_pa_t_kernel(
 
         xs = []
         load_x(0, [0])
+        vector_rows = consts.tile([P, P], BF16)
+        nc.vector.memset(vector_rows[:], 0.0)
+        for t in range(OUTPUTS):
+            for v in range(3):
+                first = BLOCKS * (3 * t + v)
+                nc.scalar.dma_start(
+                    out=vector_rows[first : first + BLOCKS, :],
+                    in_=vectors_in[t][v].rearrange("(j m) -> j m", m=P),
+                )
 
         w_codes = consts.tile([P, OUTPUTS, D], U32, align_bytes=64)
         w_scales = consts.tile([P, OUTPUTS, D], U8, align_bytes=64)
@@ -108,15 +123,6 @@ def tile_dcadecoderblock_pa_t_kernel(
                 in_=words_in[t][0].rearrange("p n t -> p (n t)").bitcast(I32),
             )
 
-        vector_rows = consts.tile([P, P], BF16)
-        nc.vector.memset(vector_rows[:], 0.0)
-        for t in range(OUTPUTS):
-            for v in range(3):
-                first = BLOCKS * (3 * t + v)
-                nc.scalar.dma_start(
-                    out=vector_rows[first : first + BLOCKS, :],
-                    in_=vectors_in[t][v].rearrange("(j m) -> j m", m=P),
-                )
         for c in range(1, CHUNKS):
             load_x(c, range(LAYERS))
 
@@ -142,6 +148,8 @@ def tile_dcadecoderblock_pa_t_kernel(
 
         stds = {}
         rstds = {}
+        shifts = {}
+        negs = {}
         parts = {}
 
         def deviation(c, l):
@@ -151,16 +159,29 @@ def tile_dcadecoderblock_pa_t_kernel(
             nc.scalar.activation(
                 out=stds[c][:, l, :], in_=mean_var[c][:, l, :, 1], func=ACT.Sqrt, bias=eps[:], scale=1.0
             )
+            if SHIFT_ON != "v":
+                if l == 0:
+                    negs[c] = small.tile([P, LAYERS, TILES], F32, name="neg")
+                nc.scalar.activation(out=negs[c][:, l, :], in_=mean_var[c][:, l, :, 0], func=ACT.Copy, scale=-1.0)
 
         def inverse(c, l):
+            if l == 0:
+                shifts[c] = small.tile([P, LAYERS, TILES], F32, name="shift")
             nc.vector.reciprocal(out=rstds[c][:, l, :], in_=stds[c][:, l, :])
+            if SHIFT_ON == "v":
+                nc.vector.scalar_tensor_tensor(
+                    out=shifts[c][:, l, :], in0=mean_var[c][:, l, :, 0], scalar=-1.0, in1=rstds[c][:, l, :],
+                    op0=ALU.mult, op1=ALU.mult,
+                )
+            else:
+                nc.gpsimd.tensor_tensor(out=shifts[c][:, l, :], in0=negs[c][:, l, :], in1=rstds[c][:, l, :], op=ALU.mult)
 
         def normalise(c, l, i):
             part = part_pool.tile([P, D], F32, name="part")
             nc.gpsimd.tensor_scalar(
                 out=part[:], in0=xs[c][:, l, i, :],
-                scalar1=mean_var[c][:, l, i, 0:1], scalar2=rstds[c][:, l, i : i + 1],
-                op0=ALU.subtract, op1=ALU.mult,
+                scalar1=rstds[c][:, l, i : i + 1], scalar2=shifts[c][:, l, i : i + 1],
+                op0=ALU.mult, op1=ALU.add,
             )
             parts[(c, l, i)] = part
 
@@ -260,29 +281,34 @@ def tile_dcadecoderblock_pa_t_kernel(
             nc.sync.dma_start(out=token_view(outs[t][b, rows, j * P : (j + 1) * P]), in_=result[:])
 
         rows_f32 = consts.tile([P, P], F32)
-        nc.vector.tensor_copy(out=rows_f32[:], in_=vector_rows[:])
-        columns_ps = turn_psum.tile([P, P], F32, tag="turn")
-        nc.tensor.transpose(columns_ps[:], rows_f32[:], ident[:])
         columns = consts.tile([P, OUTPUTS, 3, BLOCKS], F32)
-        nc.vector.tensor_copy(
-            out=columns[:].rearrange("p t v j -> p (t v j)"),
-            in_=columns_ps[:, 0 : OUTPUTS * 3 * BLOCKS],
-        )
         bias = columns[:, :, 0, :]
         gain = columns[:, :, 1, :]
         neg_bias = consts.tile([P, OUTPUTS, BLOCKS], F32)
-        nc.vector.tensor_scalar(out=neg_bias[:], in0=bias, scalar1=-1.0, scalar2=None, op0=ALU.mult)
         offset = consts.tile([P, OUTPUTS, BLOCKS], F32)
-        nc.vector.tensor_scalar(
-            out=offset[:], in0=columns[:, :, 2, :], scalar1=float(LAYERS), scalar2=None, op0=ALU.mult
-        )
-        nc.vector.scalar_tensor_tensor(
-            out=offset[:], in0=bias, scalar=float(LAYERS - 1), in1=offset[:], op0=ALU.mult, op1=ALU.add
-        )
+
+        def make_columns():
+            nc.vector.tensor_copy(out=rows_f32[:], in_=vector_rows[:])
+            columns_ps = turn_psum.tile([P, P], F32, name="columns_ps", tag="turn")
+            nc.tensor.transpose(columns_ps[:], rows_f32[:], ident[:])
+            nc.vector.tensor_copy(
+                out=columns[:].rearrange("p t v j -> p (t v j)"),
+                in_=columns_ps[:, 0 : OUTPUTS * 3 * BLOCKS],
+            )
+            nc.vector.tensor_scalar(out=neg_bias[:], in0=bias, scalar1=-1.0, scalar2=None, op0=ALU.mult)
+            nc.vector.tensor_scalar(
+                out=offset[:], in0=columns[:, :, 2, :], scalar1=float(LAYERS), scalar2=None, op0=ALU.mult
+            )
+            nc.vector.scalar_tensor_tensor(
+                out=offset[:], in0=bias, scalar=float(LAYERS - 1), in1=offset[:], op0=ALU.mult, op1=ALU.add
+            )
+
         for l in range(LAYERS):
             for half in range(HALVES):
                 turn_x(0, l, half)
                 take_x(0, l, half)
+            if l == 0:
+                make_columns()
             for i in range(TILES // 2):
                 statistics(0, l, i)
             quantise(0, l)
@@ -311,7 +337,7 @@ def tile_dcadecoderblock_pa_t_kernel(
             tile = tile_at(m + SHIFT)
             if ORDER == 1:
                 if unit_at(m - LT - 3):
-                    take_back(*units[m - LT - 3], on_vector=tail and m % 2 == 1)
+                    take_back(*units[m - LT - 3], on_vector=(tail and m % 2 == 1) or (VEXIT > 0 and not tile and not tail and m % VEXIT == 0))
                 for h in x_halves[XR * (m - 1 - XS) if m - 1 >= XS else 0 : XR * (m - XS) if m >= XS else 0]:
                     take_x(*h)
             if m == -SHIFT + 1:
@@ -330,6 +356,9 @@ def tile_dcadecoderblock_pa_t_kernel(
                 merge(*units[m - LT - 1], on_vector=tail)
             if unit_at(m):
                 multiply(*units[m], 2)
+            if m == -SHIFT:
+                for n in range(LEAD - SHIFT):
+                    multiply(*units[n], 0)
             if LEAD > 0 and unit_at(m + LEAD):
                 multiply(*units[m + LEAD], 0)
             if tile:

@@ -27,7 +27,7 @@ LAG = BLOCKS * OUTPUTS
 SHIFT = 6
 LT = 4
 PARTS = 24
-PE_EVERY = 99
+PE_EVERY = 3
 QSHIFT = 0
 ORDER = 1
 PROD = 3
@@ -36,12 +36,14 @@ SUMS = 2
 LEAD = 6
 SPREAD = 1
 XR = 1
-XS = -1
+XS = -4
 SHIFT_ON = "g"
 RB = 5
 LNB = 4
 OB = 4
 VEXIT = 0
+VM_FROM = 48
+VTAKE = 0
 FLOPS = 2 * BATCH * LAYERS * SEQ * D * D * OUTPUTS
 
 
@@ -193,14 +195,20 @@ def tile_dcadecoderblock_pa_t_kernel(
                     nc.tensor.transpose(bank[:, u, i * P : (i + 1) * P], x_words[:, u : D // 2 : 2], ident[:])
             turned_x[(c, l, half)] = bank
 
-        def take_x(c, l, half):
+        def take_x(c, l, half, on_vector=False):
             if half == 0:
                 grouped[(c, l)] = quant.tile([P, CHUNK, 4], BF16, name="grouped", align_bytes=64)
             words = grouped[(c, l)][:].rearrange("p r t -> p (r t)").bitcast(F32).rearrange("p (r u) -> p r u", u=2)
-            nc.scalar.copy(
-                out=words[:, half * HALF : (half + 1) * HALF, :],
-                in_=turned_x[(c, l, half)][:].rearrange("p u r -> p r u"),
-            )
+            if on_vector:
+                nc.vector.tensor_copy(
+                    out=words[:, half * HALF : (half + 1) * HALF, :],
+                    in_=turned_x[(c, l, half)][:].rearrange("p u r -> p r u"),
+                )
+            else:
+                nc.scalar.copy(
+                    out=words[:, half * HALF : (half + 1) * HALF, :],
+                    in_=turned_x[(c, l, half)][:].rearrange("p u r -> p r u"),
+                )
 
         def quantise(c, l):
             codes = code_pool.tile([P, CHUNK], U32, name="codes", align_bytes=64)
@@ -339,7 +347,7 @@ def tile_dcadecoderblock_pa_t_kernel(
                 if unit_at(m - LT - 3):
                     take_back(*units[m - LT - 3], on_vector=(tail and m % 2 == 1) or (VEXIT > 0 and not tile and not tail and m % VEXIT == 0))
                 for h in x_halves[XR * (m - 1 - XS) if m - 1 >= XS else 0 : XR * (m - XS) if m >= XS else 0]:
-                    take_x(*h)
+                    take_x(*h, on_vector=(VTAKE > 0 and m >= 0 and h[2] == 1 and (h[1] + h[0]) % VTAKE == 0))
             if m == -SHIFT + 1:
                 deviation(0, LAYERS - 1)
             if m == -SHIFT + 2:
@@ -352,8 +360,8 @@ def tile_dcadecoderblock_pa_t_kernel(
                 multiply(*units[m], 1)
             if tile:
                 statistics(*tile)
-            if unit_at(m - LT - 1) and (tail or (m - LT - 1) % PE_EVERY != 0):
-                merge(*units[m - LT - 1], on_vector=tail)
+            if unit_at(m - LT - 1) and (m >= VM_FROM or (m - LT - 1) % PE_EVERY != 0):
+                merge(*units[m - LT - 1], on_vector=m >= VM_FROM)
             if unit_at(m):
                 multiply(*units[m], 2)
             if m == -SHIFT:
@@ -385,7 +393,7 @@ def tile_dcadecoderblock_pa_t_kernel(
                 turn_x(*h)
             if unit_at(m - LT - 2):
                 n = m - LT - 2
-                turn_back(*units[n], merged=(n + LT + 1 >= len(units) or n % PE_EVERY != 0))
+                turn_back(*units[n], merged=(n + LT + 1 >= VM_FROM or n % PE_EVERY != 0))
             if SPREAD == 0:
                 if unit_at(m - LT + 1) and units[m - LT + 1][2] == 0:
                     turn_sums(*units[m - LT + 1][0:2], range(TILES))

@@ -33,7 +33,7 @@ ORDER = 1
 PROD = 3
 TURN = 3
 SUMS = 2
-LEAD = 6
+LEAD = 12
 SPREAD = 1
 XR = 1
 XS = -4
@@ -44,6 +44,8 @@ OB = 4
 VEXIT = 0
 VM_FROM = 48
 VTAKE = 0
+PE_UNTIL = 37
+VSUM = []
 FLOPS = 2 * BATCH * LAYERS * SEQ * D * D * OUTPUTS
 
 
@@ -244,10 +246,11 @@ def tile_dcadecoderblock_pa_t_kernel(
                 turned_sums[(c, j)] = sums_psum.tile([P, CHUNK], F32, name="turned_sums")
             bank = turned_sums[(c, j)]
             for i in tiles:
-                for l in range(LAYERS):
+                layers = [0] if c in VSUM else range(LAYERS)
+                for l in layers:
                     nc.tensor.matmul(
                         out=bank[:, i * P : (i + 1) * P], lhsT=parts[(c, l, i)][:, j * P : (j + 1) * P], rhs=ident[:],
-                        is_transpose=True, start=l == 0, stop=l == LAYERS - 1,
+                        is_transpose=True, start=l == 0, stop=l == layers[-1],
                     )
 
         def norm_term(c, j, t):
@@ -337,6 +340,9 @@ def tile_dcadecoderblock_pa_t_kernel(
         def unit_at(n):
             return units[n] if 0 <= n < len(units) else None
 
+        def on_tensor(n):
+            return n % PE_EVERY == 0 and n + LT + 1 < min(VM_FROM, PE_UNTIL)
+
         def tile_at(k):
             return x_tiles[k] if 0 <= k < len(x_tiles) else None
 
@@ -360,7 +366,7 @@ def tile_dcadecoderblock_pa_t_kernel(
                 multiply(*units[m], 1)
             if tile:
                 statistics(*tile)
-            if unit_at(m - LT - 1) and (m >= VM_FROM or (m - LT - 1) % PE_EVERY != 0):
+            if unit_at(m - LT - 1) and not on_tensor(m - LT - 1):
                 merge(*units[m - LT - 1], on_vector=m >= VM_FROM)
             if unit_at(m):
                 multiply(*units[m], 2)
@@ -379,6 +385,10 @@ def tile_dcadecoderblock_pa_t_kernel(
                 inverse(*done[0:2])
             if tile_at(m + SHIFT - 6):
                 normalise(*tile_at(m + SHIFT - 6))
+            summed = tile_at(m + SHIFT - 7)
+            if summed and summed[0] in VSUM and summed[1] > 0:
+                c3, l3, i3 = summed
+                nc.vector.tensor_tensor(out=parts[(c3, 0, i3)][:], in0=parts[(c3, 0, i3)][:], in1=parts[(c3, l3, i3)][:], op=ALU.add)
             if unit_at(m - LT):
                 norm_term(*units[m - LT])
             for k, h in enumerate(x_halves):
@@ -393,7 +403,7 @@ def tile_dcadecoderblock_pa_t_kernel(
                 turn_x(*h)
             if unit_at(m - LT - 2):
                 n = m - LT - 2
-                turn_back(*units[n], merged=(n + LT + 1 >= VM_FROM or n % PE_EVERY != 0))
+                turn_back(*units[n], merged=not on_tensor(n))
             if SPREAD == 0:
                 if unit_at(m - LT + 1) and units[m - LT + 1][2] == 0:
                     turn_sums(*units[m - LT + 1][0:2], range(TILES))

@@ -46,6 +46,8 @@ VM_FROM = 48
 VTAKE = 0
 PE_UNTIL = 37
 VSUM = []
+QB = 6
+RSQRT = 0
 FLOPS = 2 * BATCH * LAYERS * SEQ * D * D * OUTPUTS
 
 
@@ -69,7 +71,7 @@ def tile_dcadecoderblock_pa_t_kernel(
         x_pool = stack.enter_context(tc.tile_pool(name="x", bufs=CHUNKS))
         small = stack.enter_context(tc.tile_pool(name="small", bufs=3))
         part_pool = stack.enter_context(tc.tile_pool(name="part", bufs=PARTS))
-        quant = stack.enter_context(tc.tile_pool(name="quant", bufs=2 * LAYERS))
+        quant = stack.enter_context(tc.tile_pool(name="quant", bufs=QB))
         code_pool = stack.enter_context(tc.tile_pool(name="codes", bufs=CHUNKS * LAYERS))
         ln_pool = stack.enter_context(tc.tile_pool(name="ln", bufs=LNB))
         relu_pool = stack.enter_context(tc.tile_pool(name="relu", bufs=LEAD + LT + RB))
@@ -83,7 +85,7 @@ def tile_dcadecoderblock_pa_t_kernel(
         eps = consts.tile([P, 1], F32)
         nc.vector.memset(eps[:], EPS)
         warm = consts.tile([P, 1], F32)
-        nc.scalar.activation(out=warm[:], in_=eps[:], func=ACT.Sqrt)
+        nc.scalar.activation(out=warm[:], in_=eps[:], func=ACT.Abs_reciprocal_sqrt if RSQRT else ACT.Sqrt)
 
         def token_view(rows):
             return rows.rearrange("(p i) f -> p i f", i=TILES)
@@ -160,9 +162,14 @@ def tile_dcadecoderblock_pa_t_kernel(
             if l == 0:
                 stds[c] = small.tile([P, LAYERS, TILES], F32, name="std")
                 rstds[c] = small.tile([P, LAYERS, TILES], F32, name="rstd")
-            nc.scalar.activation(
-                out=stds[c][:, l, :], in_=mean_var[c][:, l, :, 1], func=ACT.Sqrt, bias=eps[:], scale=1.0
-            )
+            if RSQRT:
+                nc.scalar.activation(
+                    out=rstds[c][:, l, :], in_=mean_var[c][:, l, :, 1], func=ACT.Abs_reciprocal_sqrt, bias=eps[:], scale=1.0
+                )
+            else:
+                nc.scalar.activation(
+                    out=stds[c][:, l, :], in_=mean_var[c][:, l, :, 1], func=ACT.Sqrt, bias=eps[:], scale=1.0
+                )
             if SHIFT_ON != "v":
                 if l == 0:
                     negs[c] = small.tile([P, LAYERS, TILES], F32, name="neg")
@@ -171,7 +178,8 @@ def tile_dcadecoderblock_pa_t_kernel(
         def inverse(c, l):
             if l == 0:
                 shifts[c] = small.tile([P, LAYERS, TILES], F32, name="shift")
-            nc.vector.reciprocal(out=rstds[c][:, l, :], in_=stds[c][:, l, :])
+            if not RSQRT:
+                nc.vector.reciprocal(out=rstds[c][:, l, :], in_=stds[c][:, l, :])
             if SHIFT_ON == "v":
                 nc.vector.scalar_tensor_tensor(
                     out=shifts[c][:, l, :], in0=mean_var[c][:, l, :, 0], scalar=-1.0, in1=rstds[c][:, l, :],
@@ -298,10 +306,16 @@ def tile_dcadecoderblock_pa_t_kernel(
         neg_bias = consts.tile([P, OUTPUTS, BLOCKS], F32)
         offset = consts.tile([P, OUTPUTS, BLOCKS], F32)
 
-        def make_columns():
+        turned_rows = []
+
+        def make_rows():
             nc.vector.tensor_copy(out=rows_f32[:], in_=vector_rows[:])
             columns_ps = turn_psum.tile([P, P], F32, name="columns_ps", tag="turn")
             nc.tensor.transpose(columns_ps[:], rows_f32[:], ident[:])
+            turned_rows.append(columns_ps)
+
+        def make_columns():
+            columns_ps = turned_rows[0]
             nc.vector.tensor_copy(
                 out=columns[:].rearrange("p t v j -> p (t v j)"),
                 in_=columns_ps[:, 0 : OUTPUTS * 3 * BLOCKS],
@@ -318,15 +332,18 @@ def tile_dcadecoderblock_pa_t_kernel(
             for half in range(HALVES):
                 turn_x(0, l, half)
                 take_x(0, l, half)
-            if l == 0:
-                make_columns()
+        for l in range(LAYERS):
             for i in range(TILES // 2):
                 statistics(0, l, i)
+            if l == 1:
+                make_columns()
             quantise(0, l)
             for i in range(TILES // 2, TILES):
                 statistics(0, l, i)
             for i in range(TILES):
                 aggregate(0, l, i)
+            if l == 0:
+                make_rows()
             if l > 0:
                 deviation(0, l - 1)
                 inverse(0, l - 1)

@@ -48,6 +48,12 @@ PE_UNTIL = 37
 VSUM = []
 QB = 6
 RSQRT = 0
+THIRD_ON_V = 0
+NEG_ON_G = 0
+LAST = 0
+CNUM = 1
+CDEN = 2
+CSP = 3
 FLOPS = 2 * BATCH * LAYERS * SEQ * D * D * OUTPUTS
 
 
@@ -173,7 +179,12 @@ def tile_dcadecoderblock_pa_t_kernel(
             if SHIFT_ON != "v":
                 if l == 0:
                     negs[c] = small.tile([P, LAYERS, TILES], F32, name="neg")
-                nc.scalar.activation(out=negs[c][:, l, :], in_=mean_var[c][:, l, :, 0], func=ACT.Copy, scale=-1.0)
+                if NEG_ON_G:
+                    nc.gpsimd.tensor_scalar(
+                        out=negs[c][:, l, :], in0=mean_var[c][:, l, :, 0], scalar1=-1.0, scalar2=0.0, op0=ALU.mult, op1=ALU.add
+                    )
+                else:
+                    nc.scalar.activation(out=negs[c][:, l, :], in_=mean_var[c][:, l, :, 0], func=ACT.Copy, scale=-1.0)
 
         def inverse(c, l):
             if l == 0:
@@ -363,14 +374,36 @@ def tile_dcadecoderblock_pa_t_kernel(
         def tile_at(k):
             return x_tiles[k] if 0 <= k < len(x_tiles) else None
 
-        for m in range(-SHIFT, len(units) + LT + 4):
+        catch = (CHUNKS - 1) * BLOCKS * OUTPUTS
+
+        def term_round(n):
+            return n + LT if n < catch else max(n + LAST, catch + LT + ((n - catch) * CNUM) // CDEN)
+
+        def merge_round(n):
+            return max(term_round(n), n) + 1
+
+        terms_at = {}
+        merges_at = {}
+        sums_at = {}
+        for n in range(len(units)):
+            terms_at.setdefault(term_round(n), []).append(n)
+            merges_at.setdefault(merge_round(n), []).append(n)
+            if n % OUTPUTS == 0:
+                pieces = ((3, [0]), (2, [1]), (1, [2, 3])) if n < catch + CSP else ((2, [0, 1]), (1, [2, 3]))
+                for back, tiles in pieces:
+                    sums_at.setdefault(term_round(n) - back, []).append((n, tiles))
+        last_round = merge_round(len(units) - 1) + 2
+
+        def on_pe(n):
+            return n % PE_EVERY == 0 and merge_round(n) < min(VM_FROM, PE_UNTIL)
+
+        for m in range(-SHIFT, last_round + 1):
             tail = m >= len(units)
             tile = tile_at(m + SHIFT)
-            if ORDER == 1:
-                if unit_at(m - LT - 3):
-                    take_back(*units[m - LT - 3], on_vector=(tail and m % 2 == 1) or (VEXIT > 0 and not tile and not tail and m % VEXIT == 0))
-                for h in x_halves[XR * (m - 1 - XS) if m - 1 >= XS else 0 : XR * (m - XS) if m >= XS else 0]:
-                    take_x(*h, on_vector=(VTAKE > 0 and m >= 0 and h[2] == 1 and (h[1] + h[0]) % VTAKE == 0))
+            for k, n in enumerate(merges_at.get(m - 2, [])):
+                take_back(*units[n], on_vector=tail and (m + k) % 2 == 1)
+            for h in x_halves[XR * (m - 1 - XS) if m - 1 >= XS else 0 : XR * (m - XS) if m >= XS else 0]:
+                take_x(*h)
             if m == -SHIFT + 1:
                 deviation(0, LAYERS - 1)
             if m == -SHIFT + 2:
@@ -378,19 +411,18 @@ def tile_dcadecoderblock_pa_t_kernel(
                 for i in range(TILES):
                     normalise(0, LAYERS - 1, i)
             if unit_at(m):
-                if LEAD == 0:
-                    multiply(*units[m], 0)
                 multiply(*units[m], 1)
             if tile:
                 statistics(*tile)
-            if unit_at(m - LT - 1) and not on_tensor(m - LT - 1):
-                merge(*units[m - LT - 1], on_vector=m >= VM_FROM)
+            for n in merges_at.get(m, []):
+                if not on_pe(n):
+                    merge(*units[n], on_vector=m >= VM_FROM)
             if unit_at(m):
                 multiply(*units[m], 2)
             if m == -SHIFT:
                 for n in range(LEAD - SHIFT):
                     multiply(*units[n], 0)
-            if LEAD > 0 and unit_at(m + LEAD):
+            if unit_at(m + LEAD):
                 multiply(*units[m + LEAD], 0)
             if tile:
                 aggregate(*tile)
@@ -406,25 +438,14 @@ def tile_dcadecoderblock_pa_t_kernel(
             if summed and summed[0] in VSUM and summed[1] > 0:
                 c3, l3, i3 = summed
                 nc.vector.tensor_tensor(out=parts[(c3, 0, i3)][:], in0=parts[(c3, 0, i3)][:], in1=parts[(c3, l3, i3)][:], op=ALU.add)
-            if unit_at(m - LT):
-                norm_term(*units[m - LT])
+            for n in terms_at.get(m, []):
+                norm_term(*units[n])
             for k, h in enumerate(x_halves):
                 if h[2] == HALVES - 1 and k // XR + XS + 2 == m:
                     quantise(*h[0:2])
-            if ORDER == 0:
-                if 0 < m <= len(x_halves):
-                    take_x(*x_halves[m - 1])
-                if unit_at(m - LT - 3):
-                    take_back(*units[m - LT - 3], on_vector=tail and m % 2 == 1)
             for h in x_halves[XR * (m - XS) if m >= XS else 0 : XR * (m + 1 - XS) if m + 1 >= XS else 0]:
                 turn_x(*h)
-            if unit_at(m - LT - 2):
-                n = m - LT - 2
-                turn_back(*units[n], merged=not on_tensor(n))
-            if SPREAD == 0:
-                if unit_at(m - LT + 1) and units[m - LT + 1][2] == 0:
-                    turn_sums(*units[m - LT + 1][0:2], range(TILES))
-            else:
-                for back, tiles in ((3, [0]), (2, [1]), (1, [2, 3])):
-                    if unit_at(m - LT + back) and units[m - LT + back][2] == 0:
-                        turn_sums(*units[m - LT + back][0:2], tiles)
+            for n in merges_at.get(m - 1, []):
+                turn_back(*units[n], merged=not on_pe(n))
+            for n, tiles in sums_at.get(m, []):
+                turn_sums(*units[n][0:2], tiles)

@@ -24,8 +24,8 @@ HALVES = CHUNK // HALF
 OUTPUTS = 3
 LAG = BLOCKS * OUTPUTS
 
-SHIFT = 6
-LT = 4
+SHIFT = 5
+LT = 3
 PARTS = 24
 PE_EVERY = 3
 QSHIFT = 0
@@ -36,7 +36,7 @@ SUMS = 2
 LEAD = 12
 SPREAD = 1
 XR = 1
-XS = -4
+XS = -5
 SHIFT_ON = "g"
 RB = 5
 LNB = 4
@@ -44,16 +44,33 @@ OB = 4
 VEXIT = 0
 VM_FROM = 48
 VTAKE = 0
-PE_UNTIL = 37
+PE_UNTIL = 42
 VSUM = []
 QB = 6
-RSQRT = 0
+RSQRT = 1
 THIRD_ON_V = 0
 NEG_ON_G = 0
 LAST = 0
 CNUM = 1
 CDEN = 2
 CSP = 3
+XSTEP = 1.0
+CHAIN = []
+VNORM = [(3, 1)]
+VN0 = 32
+HEADS = (0, 2, 4, 8)
+PIECES = ((3, 0, 4), (2, 4, 8), (1, 8, 12))
+PIECES2 = ((2, 0, 6), (1, 6, 12))
+NPE = 1
+NPE_LATE = 1
+ORD = 1
+R0FIRST = 2
+BACKFIRST = 1
+NORM_AT = 0
+VNRATE = 1
+GLN = []
+EV = 0
+NMLAG = 5
 FLOPS = 2 * BATCH * LAYERS * SEQ * D * D * OUTPUTS
 
 
@@ -108,16 +125,21 @@ def tile_dcadecoderblock_pa_t_kernel(
                 nc.sync.dma_start(out=xs[c][:, l], in_=token_view(layer_outputs[b, l, rows, :]))
 
         xs = []
-        load_x(0, [0])
-        vector_rows = consts.tile([P, P], BF16)
-        nc.vector.memset(vector_rows[:], 0.0)
-        for t in range(OUTPUTS):
-            for v in range(3):
-                first = BLOCKS * (3 * t + v)
-                nc.scalar.dma_start(
-                    out=vector_rows[first : first + BLOCKS, :],
-                    in_=vectors_in[t][v].rearrange("(j m) -> j m", m=P),
-                )
+        load_x(0, range(LAYERS))
+        bias_rows = consts.tile([P, P], BF16)
+        norm_rows = consts.tile([P, P], BF16)
+        nc.vector.memset(bias_rows[:], 0.0)
+
+        def load_vectors(rows, first_vector, vectors):
+            for v in vectors:
+                for t in range(OUTPUTS):
+                    first = BLOCKS * (OUTPUTS * (v - first_vector) + t)
+                    nc.sync.dma_start(
+                        out=rows[first : first + BLOCKS, :],
+                        in_=vectors_in[t][v].rearrange("(j m) -> j m", m=P),
+                    )
+
+        load_vectors(bias_rows, 0, [0])
 
         w_codes = consts.tile([P, OUTPUTS, D], U32, align_bytes=64)
         w_scales = consts.tile([P, OUTPUTS, D], U8, align_bytes=64)
@@ -128,14 +150,15 @@ def tile_dcadecoderblock_pa_t_kernel(
                     out=w_scales[32 * quadrant : 32 * quadrant + 4, t, :].bitcast(I32),
                     in_=scales_in[t][0, 4 * quadrant : 4 * quadrant + 4, :].bitcast(I32),
                 )
-        load_x(0, [1, 2])
-        for t in range(OUTPUTS):
             nc.sync.dma_start(
                 out=w_codes[:, t, :].bitcast(I32),
                 in_=words_in[t][0].rearrange("p n t -> p (n t)").bitcast(I32),
             )
 
-        for c in range(1, CHUNKS):
+        nc.vector.memset(norm_rows[:], 0.0)
+        load_x(1, range(LAYERS))
+        load_vectors(norm_rows, 1, [1, 2])
+        for c in range(2, CHUNKS):
             load_x(c, range(LAYERS))
 
         six = {}
@@ -249,7 +272,7 @@ def tile_dcadecoderblock_pa_t_kernel(
                 rhs=codes[:].bitcast(FP8X4), rhs_scale=scales[:],
                 start=True, stop=True,
             )
-            if l == 0:
+            if l == 0 and units.index((c, j, t)) not in CHAIN:
                 relu_sums[(c, j, t)] = relu_pool.tile([P, CHUNK], F32, name="relu")
                 nc.scalar.activation(
                     out=relu_sums[(c, j, t)][:], in_=prod[:], func=ACT.Relu, bias=bias[:, t, j : j + 1], scale=1.0
@@ -260,36 +283,54 @@ def tile_dcadecoderblock_pa_t_kernel(
                     in1=relu_sums[(c, j, t)][:], op0=ALU.max, op1=ALU.add,
                 )
 
-        def turn_sums(c, j, tiles):
-            if tiles[0] == 0:
+        def sum_steps(c):
+            layers = [l for l in range(LAYERS) if (c, l) not in VNORM]
+            return [(i, l, layers) for i in range(TILES) for l in layers]
+
+        def turn_sums(c, j, first, last):
+            if first == 0:
                 turned_sums[(c, j)] = sums_psum.tile([P, CHUNK], F32, name="turned_sums")
             bank = turned_sums[(c, j)]
-            for i in tiles:
-                layers = [0] if c in VSUM else range(LAYERS)
-                for l in layers:
+            steps = sum_steps(c)
+            for i, l, layers in steps[len(steps) * first // 12 : len(steps) * last // 12]:
+                if True:
                     nc.tensor.matmul(
                         out=bank[:, i * P : (i + 1) * P], lhsT=parts[(c, l, i)][:, j * P : (j + 1) * P], rhs=ident[:],
                         is_transpose=True, start=l == 0, stop=l == layers[-1],
                     )
 
         def norm_term(c, j, t):
-            ln = ln_pool.tile([P, CHUNK], F32, name="ln")
-            nc.scalar.activation(
-                out=ln[:], in_=turned_sums[(c, j)][:], func=ACT.Identity,
-                scale=gain[:, t, j : j + 1], bias=offset[:, t, j : j + 1],
-            )
-            norm_terms[(c, j, t)] = ln
+            n = units.index((c, j, t))
+            if n in CHAIN:
+                ln = relu_pool.tile([P, CHUNK], F32, name="relu")
+                relu_sums[(c, j, t)] = ln
+            else:
+                ln = ln_pool.tile([P, CHUNK], F32, name="ln")
+                norm_terms[(c, j, t)] = ln
+            shift_by = offset3 if n in CHAIN else offset
+            if n in GLN:
+                nc.gpsimd.tensor_scalar(
+                    out=ln[:], in0=flat_sums[(c, j)][:], scalar1=gain[:, t, j : j + 1], scalar2=shift_by[:, t, j : j + 1],
+                    op0=ALU.mult, op1=ALU.add,
+                )
+            else:
+                nc.scalar.activation(
+                    out=ln[:], in_=turned_sums[(c, j)][:], func=ACT.Identity,
+                    scale=gain[:, t, j : j + 1], bias=shift_by[:, t, j : j + 1],
+                )
 
-        def merge(c, j, t, on_vector):
+        def merge(c, j, t, on_vector, npe):
             engine = nc.vector if on_vector else nc.gpsimd
+            cols = slice(npe * P, CHUNK)
             engine.tensor_tensor(
-                out=relu_sums[(c, j, t)][:], in0=relu_sums[(c, j, t)][:], in1=norm_terms[(c, j, t)][:], op=ALU.add
+                out=relu_sums[(c, j, t)][:, cols], in0=relu_sums[(c, j, t)][:, cols], in1=norm_terms[(c, j, t)][:, cols], op=ALU.add
             )
 
-        def turn_back(c, j, t, merged):
+        def turn_back(c, j, t, npe):
             bank = turn_psum.tile([P, TILES, P], F32, name="back", tag="turn")
             for i in range(TILES):
                 tokens = slice(i * P, (i + 1) * P)
+                merged = i >= npe
                 nc.tensor.matmul(
                     out=bank[:, i, :], lhsT=relu_sums[(c, j, t)][:, tokens], rhs=ident[:],
                     is_transpose=True, start=True, stop=merged,
@@ -311,57 +352,89 @@ def tile_dcadecoderblock_pa_t_kernel(
             nc.sync.dma_start(out=token_view(outs[t][b, rows, j * P : (j + 1) * P]), in_=result[:])
 
         rows_f32 = consts.tile([P, P], F32)
-        columns = consts.tile([P, OUTPUTS, 3, BLOCKS], F32)
-        bias = columns[:, :, 0, :]
-        gain = columns[:, :, 1, :]
+        norm_f32 = consts.tile([P, P], F32)
+        bias = consts.tile([P, OUTPUTS, BLOCKS], F32)
+        columns = consts.tile([P, 2, OUTPUTS, BLOCKS], F32)
+        gain = columns[:, 0, :, :]
         neg_bias = consts.tile([P, OUTPUTS, BLOCKS], F32)
         offset = consts.tile([P, OUTPUTS, BLOCKS], F32)
 
+        offset3 = consts.tile([P, OUTPUTS, BLOCKS], F32)
+        flat_sums = {}
         turned_rows = []
 
         def make_rows():
-            nc.vector.tensor_copy(out=rows_f32[:], in_=vector_rows[:])
+            nc.vector.tensor_copy(out=rows_f32[:], in_=bias_rows[:])
             columns_ps = turn_psum.tile([P, P], F32, name="columns_ps", tag="turn")
             nc.tensor.transpose(columns_ps[:], rows_f32[:], ident[:])
             turned_rows.append(columns_ps)
 
         def make_columns():
-            columns_ps = turned_rows[0]
             nc.vector.tensor_copy(
-                out=columns[:].rearrange("p t v j -> p (t v j)"),
-                in_=columns_ps[:, 0 : OUTPUTS * 3 * BLOCKS],
+                out=bias[:].rearrange("p t j -> p (t j)"), in_=turned_rows[0][:, 0 : OUTPUTS * BLOCKS]
             )
-            nc.vector.tensor_scalar(out=neg_bias[:], in0=bias, scalar1=-1.0, scalar2=None, op0=ALU.mult)
+            nc.vector.tensor_scalar(out=neg_bias[:], in0=bias[:], scalar1=-1.0, scalar2=None, op0=ALU.mult)
+
+        def make_norm_rows():
+            columns_ps = turn_psum.tile([P, P], F32, name="columns_ps", tag="turn")
+            nc.tensor.transpose(columns_ps[:], norm_f32[:], ident[:])
+            turned_rows.append(columns_ps)
+
+        def make_norm_columns():
+            nc.vector.tensor_copy(
+                out=columns[:].rearrange("p v t j -> p (v t j)"), in_=turned_rows[1][:, 0 : 2 * OUTPUTS * BLOCKS]
+            )
             nc.vector.tensor_scalar(
-                out=offset[:], in0=columns[:, :, 2, :], scalar1=float(LAYERS), scalar2=None, op0=ALU.mult
+                out=offset[:], in0=columns[:, 1, :, :], scalar1=float(LAYERS), scalar2=None, op0=ALU.mult
             )
             nc.vector.scalar_tensor_tensor(
-                out=offset[:], in0=bias, scalar=float(LAYERS - 1), in1=offset[:], op0=ALU.mult, op1=ALU.add
+                out=offset[:], in0=bias[:], scalar=float(LAYERS - 1), in1=offset[:], op0=ALU.mult, op1=ALU.add
             )
+            if CHAIN:
+                nc.vector.tensor_tensor(out=offset3[:], in0=offset[:], in1=bias[:], op=ALU.add)
 
+        def flatten_sums(c, j):
+            flat = ln_pool.tile([P, CHUNK], F32, name="flat")
+            if EV:
+                nc.vector.tensor_copy(out=flat[:], in_=turned_sums[(c, j)][:])
+            else:
+                nc.scalar.copy(out=flat[:], in_=turned_sums[(c, j)][:])
+            flat_sums[(c, j)] = flat
+
+        units = [(c, j, t) for c in range(CHUNKS) for j in range(BLOCKS) for t in range(OUTPUTS)]
+        firsts = [n for n in range(len(units)) if n not in CHAIN]
         for l in range(LAYERS):
             for half in range(HALVES):
                 turn_x(0, l, half)
                 take_x(0, l, half)
-        for l in range(LAYERS):
-            for i in range(TILES // 2):
-                statistics(0, l, i)
-            if l == 1:
-                make_columns()
+        def first_relus(a, b):
+            for k in range(a, b):
+                multiply(*head_units[k], 0)
+
+        head_units = [(0, j, t) for t in range(OUTPUTS) for j in range(BLOCKS)] + [units[n] for n in firsts[12:]]
+        for i in range(3):
+            statistics(0, 0, i)
+        make_rows()
+        quantise(0, 0)
+        statistics(0, 0, 3)
+        make_columns()
+        for i in range(TILES):
+            aggregate(0, 0, i)
+        for l in range(1, LAYERS):
+            first_relus(HEADS[l - 1], HEADS[l])
+            deviation(0, l - 1)
+            statistics(0, l, 0)
             quantise(0, l)
-            for i in range(TILES // 2, TILES):
+            inverse(0, l - 1)
+            for i in range(TILES):
+                normalise(0, l - 1, i)
+            for i in range(1, TILES):
                 statistics(0, l, i)
             for i in range(TILES):
                 aggregate(0, l, i)
-            if l == 0:
-                make_rows()
-            if l > 0:
-                deviation(0, l - 1)
-                inverse(0, l - 1)
-                for i in range(TILES):
-                    normalise(0, l - 1, i)
+        first_relus(HEADS[2], HEADS[3])
+        nc.vector.tensor_copy(out=norm_f32[:], in_=norm_rows[:])
 
-        units = [(c, j, t) for c in range(CHUNKS) for j in range(BLOCKS) for t in range(OUTPUTS)]
         x_halves = [(c, l, half) for c in range(1, CHUNKS) for l in range(LAYERS) for half in range(HALVES)]
         x_tiles = [(c, l, i) for c in range(1, CHUNKS) for l in range(LAYERS) for i in range(TILES)]
 
@@ -377,10 +450,12 @@ def tile_dcadecoderblock_pa_t_kernel(
         catch = (CHUNKS - 1) * BLOCKS * OUTPUTS
 
         def term_round(n):
+            if n in CHAIN:
+                return n - 1
             return n + LT if n < catch else max(n + LAST, catch + LT + ((n - catch) * CNUM) // CDEN)
 
         def merge_round(n):
-            return max(term_round(n), n) + 1
+            return max(term_round(n) + 1, n + 1) if n not in CHAIN else n
 
         terms_at = {}
         merges_at = {}
@@ -389,41 +464,76 @@ def tile_dcadecoderblock_pa_t_kernel(
             terms_at.setdefault(term_round(n), []).append(n)
             merges_at.setdefault(merge_round(n), []).append(n)
             if n % OUTPUTS == 0:
-                pieces = ((3, [0]), (2, [1]), (1, [2, 3])) if n < catch + CSP else ((2, [0, 1]), (1, [2, 3]))
-                for back, tiles in pieces:
-                    sums_at.setdefault(term_round(n) - back, []).append((n, tiles))
+                pieces = PIECES if n < catch + CSP else PIECES2
+                for back, first, last in pieces:
+                    sums_at.setdefault(term_round(n) - back, []).append((n, first, last))
         last_round = merge_round(len(units) - 1) + 2
 
-        def on_pe(n):
-            return n % PE_EVERY == 0 and merge_round(n) < min(VM_FROM, PE_UNTIL)
+        def npe_of(n):
+            if n in CHAIN:
+                return 0
+            if merge_round(n) >= VM_FROM:
+                return 0
+            if NPE < 0:
+                return TILES if n % PE_EVERY == 0 and merge_round(n) < PE_UNTIL else 0
+            return NPE if merge_round(n) < PE_UNTIL else NPE_LATE
+
+        def x_round(k):
+            return XS + k if k < 6 else XS + 6 + int((k - 6) * XSTEP)
+
+        x_at = {}
+        for k, h in enumerate(x_halves):
+            x_at.setdefault(x_round(k), []).append(h)
+        firsts_at = {}
+        for k in range(HEADS[3], len(firsts)):
+            r = k - LEAD if k >= min(LEAD, 12) else -SHIFT + ((k - HEADS[3]) * (12 - LEAD + SHIFT)) // (12 - HEADS[3])
+            firsts_at.setdefault(r, []).append(k)
+
+        vnorms = [(c, l, i) for c in range(CHUNKS) for i in range(TILES) for l in range(1, LAYERS) if (c, l) in VNORM]
+        def r0s(m):
+            for k in firsts_at.get(m, []):
+                multiply(*head_units[k], 0)
+
+        def terms(m):
+            for n in terms_at.get(m, []):
+                if n % OUTPUTS == 0 and any(k in GLN for k in range(n, n + OUTPUTS)):
+                    flatten_sums(*units[n][0:2])
+                norm_term(*units[n])
 
         for m in range(-SHIFT, last_round + 1):
             tail = m >= len(units)
             tile = tile_at(m + SHIFT)
             for k, n in enumerate(merges_at.get(m - 2, [])):
                 take_back(*units[n], on_vector=tail and (m + k) % 2 == 1)
-            for h in x_halves[XR * (m - 1 - XS) if m - 1 >= XS else 0 : XR * (m - XS) if m >= XS else 0]:
+            for h in x_at.get(m - 1, []):
                 take_x(*h)
+            if ORD == 1 or (ORD == 2 and not x_at.get(m - 1)):
+                terms(m)
             if m == -SHIFT + 1:
                 deviation(0, LAYERS - 1)
             if m == -SHIFT + 2:
                 inverse(0, LAYERS - 1)
                 for i in range(TILES):
                     normalise(0, LAYERS - 1, i)
+            if m in CHAIN:
+                multiply(*units[m], 0)
+            if R0FIRST == 1:
+                r0s(m)
             if unit_at(m):
                 multiply(*units[m], 1)
             if tile:
                 statistics(*tile)
+            if R0FIRST == 2:
+                r0s(m)
             for n in merges_at.get(m, []):
-                if not on_pe(n):
-                    merge(*units[n], on_vector=m >= VM_FROM)
+                if npe_of(n) < TILES and n not in CHAIN:
+                    merge(*units[n], m >= VM_FROM, npe_of(n))
             if unit_at(m):
                 multiply(*units[m], 2)
-            if m == -SHIFT:
-                for n in range(LEAD - SHIFT):
-                    multiply(*units[n], 0)
-            if unit_at(m + LEAD):
-                multiply(*units[m + LEAD], 0)
+            if R0FIRST == 0:
+                r0s(m)
+            if m == NORM_AT:
+                make_norm_columns()
             if tile:
                 aggregate(*tile)
             done = tile_at(m + SHIFT - 1)
@@ -432,20 +542,43 @@ def tile_dcadecoderblock_pa_t_kernel(
             done = tile_at(m + SHIFT - 2)
             if done and done[2] == TILES - 1:
                 inverse(*done[0:2])
-            if tile_at(m + SHIFT - 6):
-                normalise(*tile_at(m + SHIFT - 6))
+            tn = tile_at(m + SHIFT - NMLAG)
+            if tn and (tn[0], tn[1]) not in VNORM and not (tn[1] == 0 and (tn[0], 1) in VNORM):
+                normalise(*tn)
+            if tn and tn[2] == TILES - 1 and (tn[0], tn[1]) in VNORM and (tn[0], tn[1] + 1) not in VNORM:
+                c3 = tn[0]
+                for l3 in range(1, tn[1] + 1):
+                    nc.gpsimd.tensor_tensor(out=shifts[c3][:, 0, :], in0=shifts[c3][:, 0, :], in1=shifts[c3][:, l3, :], op=ALU.add)
+                for i3 in range(TILES):
+                    normalise(c3, 0, i3)
+            if m >= VN0:
+                for c3, l3, i3 in vnorms[VNRATE * (m - VN0) : VNRATE * (m - VN0 + 1)]:
+                    nc.vector.scalar_tensor_tensor(
+                        out=parts[(c3, 0, i3)][:], in0=xs[c3][:, l3, i3, :], scalar=rstds[c3][:, l3, i3 : i3 + 1],
+                        in1=parts[(c3, 0, i3)][:], op0=ALU.mult, op1=ALU.add,
+                    )
             summed = tile_at(m + SHIFT - 7)
             if summed and summed[0] in VSUM and summed[1] > 0:
                 c3, l3, i3 = summed
                 nc.vector.tensor_tensor(out=parts[(c3, 0, i3)][:], in0=parts[(c3, 0, i3)][:], in1=parts[(c3, l3, i3)][:], op=ALU.add)
-            for n in terms_at.get(m, []):
+            if ORD == 0 or (ORD == 2 and x_at.get(m - 1)):
+                terms(m)
+            for n in []:
+                if n % OUTPUTS == 0 and any(k in GLN for k in range(n, n + OUTPUTS)):
+                    flatten_sums(*units[n][0:2])
                 norm_term(*units[n])
             for k, h in enumerate(x_halves):
-                if h[2] == HALVES - 1 and k // XR + XS + 2 == m:
+                if h[2] == HALVES - 1 and x_round(k) + 2 == m:
                     quantise(*h[0:2])
-            for h in x_halves[XR * (m - XS) if m >= XS else 0 : XR * (m + 1 - XS) if m + 1 >= XS else 0]:
-                turn_x(*h)
+            if m == NORM_AT - 1:
+                make_norm_rows()
+            if BACKFIRST == 0:
+                for h in x_at.get(m, []):
+                    turn_x(*h)
             for n in merges_at.get(m - 1, []):
-                turn_back(*units[n], merged=not on_pe(n))
-            for n, tiles in sums_at.get(m, []):
-                turn_sums(*units[n][0:2], tiles)
+                turn_back(*units[n], npe_of(n))
+            for n, first, last in sums_at.get(m, []):
+                turn_sums(*units[n][0:2], first, last)
+            if BACKFIRST == 1:
+                for h in x_at.get(m, []):
+                    turn_x(*h)

@@ -64,6 +64,10 @@ PIECES2 = ((2, 0, 6), (1, 6, 12))
 NPE = 1
 NPE_LATE = 1
 ORD = 1
+SHARE = 1
+BCV = list(range(0, 46, 4))
+VNLAG = 1
+VNSTEP = 1
 R0FIRST = 2
 BACKFIRST = 1
 NORM_AT = 0
@@ -99,7 +103,7 @@ def tile_dcadecoderblock_pa_t_kernel(
         ln_pool = stack.enter_context(tc.tile_pool(name="ln", bufs=LNB))
         relu_pool = stack.enter_context(tc.tile_pool(name="relu", bufs=LEAD + LT + RB))
         out_pool = stack.enter_context(tc.tile_pool(name="out", bufs=OB))
-        prod_psum = stack.enter_context(tc.psum_pool(name="prod", bufs=PROD))
+        prod_psum = stack.enter_context(tc.psum_pool(name="prod", bufs=PROD + TURN * SHARE))
         turn_psum = stack.enter_context(tc.psum_pool(name="turn", bufs=TURN))
         sums_psum = stack.enter_context(tc.psum_pool(name="sums", bufs=SUMS))
 
@@ -232,7 +236,7 @@ def tile_dcadecoderblock_pa_t_kernel(
             parts[(c, l, i)] = part
 
         def turn_x(c, l, half):
-            bank = turn_psum.tile([P, 2, HALF], F32, name="turned_x", tag="turn")
+            bank = (prod_psum if SHARE else turn_psum).tile([P, 2, HALF], F32, name="turned_x", tag="bank" if SHARE else "turn")
             for i in range(HALF // P):
                 x_words = xs[c][:, l, half * (HALF // P) + i, :].bitcast(F32)
                 for u in range(2):
@@ -265,7 +269,7 @@ def tile_dcadecoderblock_pa_t_kernel(
         def multiply(c, j, t, l):
             block = slice(j * P, (j + 1) * P)
             codes, scales = operands[(c, l)]
-            prod = prod_psum.tile([P, CHUNK], F32, name="prod")
+            prod = prod_psum.tile([P, CHUNK], F32, name="prod", tag="bank" if SHARE else "prod")
             nc.tensor.matmul_mx(
                 out=prod[:],
                 lhsT=w_codes[:, t, block].bitcast(FP8X4), lhsT_scale=w_scales[:, t, block],
@@ -327,7 +331,7 @@ def tile_dcadecoderblock_pa_t_kernel(
             )
 
         def turn_back(c, j, t, npe):
-            bank = turn_psum.tile([P, TILES, P], F32, name="back", tag="turn")
+            bank = (prod_psum if SHARE else turn_psum).tile([P, TILES, P], F32, name="back", tag="bank" if SHARE else "turn")
             for i in range(TILES):
                 tokens = slice(i * P, (i + 1) * P)
                 merged = i >= npe
@@ -365,7 +369,7 @@ def tile_dcadecoderblock_pa_t_kernel(
 
         def make_rows():
             nc.vector.tensor_copy(out=rows_f32[:], in_=bias_rows[:])
-            columns_ps = turn_psum.tile([P, P], F32, name="columns_ps", tag="turn")
+            columns_ps = (prod_psum if SHARE else turn_psum).tile([P, P], F32, name="columns_ps", tag="bank" if SHARE else "turn")
             nc.tensor.transpose(columns_ps[:], rows_f32[:], ident[:])
             turned_rows.append(columns_ps)
 
@@ -376,7 +380,7 @@ def tile_dcadecoderblock_pa_t_kernel(
             nc.vector.tensor_scalar(out=neg_bias[:], in0=bias[:], scalar1=-1.0, scalar2=None, op0=ALU.mult)
 
         def make_norm_rows():
-            columns_ps = turn_psum.tile([P, P], F32, name="columns_ps", tag="turn")
+            columns_ps = (prod_psum if SHARE else turn_psum).tile([P, P], F32, name="columns_ps", tag="bank" if SHARE else "turn")
             nc.tensor.transpose(columns_ps[:], norm_f32[:], ident[:])
             turned_rows.append(columns_ps)
 
@@ -489,7 +493,11 @@ def tile_dcadecoderblock_pa_t_kernel(
             r = k - LEAD if k >= min(LEAD, 12) else -SHIFT + ((k - HEADS[3]) * (12 - LEAD + SHIFT)) // (12 - HEADS[3])
             firsts_at.setdefault(r, []).append(k)
 
-        vnorms = [(c, l, i) for c in range(CHUNKS) for i in range(TILES) for l in range(1, LAYERS) if (c, l) in VNORM]
+        vn_at = {}
+        for c, l in VNORM:
+            base = (12 * (c - 1) + 4 * l + 3) - SHIFT + NMLAG
+            for i in range(TILES):
+                vn_at.setdefault(base + VNLAG + (i * VNSTEP if l == 1 else i), []).append((c, l, i))
         def r0s(m):
             for k in firsts_at.get(m, []):
                 multiply(*head_units[k], 0)
@@ -504,7 +512,7 @@ def tile_dcadecoderblock_pa_t_kernel(
             tail = m >= len(units)
             tile = tile_at(m + SHIFT)
             for k, n in enumerate(merges_at.get(m - 2, [])):
-                take_back(*units[n], on_vector=tail and (m + k) % 2 == 1)
+                take_back(*units[n], on_vector=tail and (m + k) % 2 == 1 or m < len(units) and n in BCV)
             for h in x_at.get(m - 1, []):
                 take_x(*h)
             if ORD == 1 or (ORD == 2 and not x_at.get(m - 1)):
@@ -551,16 +559,11 @@ def tile_dcadecoderblock_pa_t_kernel(
                     nc.gpsimd.tensor_tensor(out=shifts[c3][:, 0, :], in0=shifts[c3][:, 0, :], in1=shifts[c3][:, l3, :], op=ALU.add)
                 for i3 in range(TILES):
                     normalise(c3, 0, i3)
-            if m >= VN0:
-                for c3, l3, i3 in vnorms[VNRATE * (m - VN0) : VNRATE * (m - VN0 + 1)]:
-                    nc.vector.scalar_tensor_tensor(
-                        out=parts[(c3, 0, i3)][:], in0=xs[c3][:, l3, i3, :], scalar=rstds[c3][:, l3, i3 : i3 + 1],
-                        in1=parts[(c3, 0, i3)][:], op0=ALU.mult, op1=ALU.add,
-                    )
-            summed = tile_at(m + SHIFT - 7)
-            if summed and summed[0] in VSUM and summed[1] > 0:
-                c3, l3, i3 = summed
-                nc.vector.tensor_tensor(out=parts[(c3, 0, i3)][:], in0=parts[(c3, 0, i3)][:], in1=parts[(c3, l3, i3)][:], op=ALU.add)
+            for c3, l3, i3 in vn_at.get(m, []):
+                nc.vector.scalar_tensor_tensor(
+                    out=parts[(c3, 0, i3)][:], in0=xs[c3][:, l3, i3, :], scalar=rstds[c3][:, l3, i3 : i3 + 1],
+                    in1=parts[(c3, 0, i3)][:], op0=ALU.mult, op1=ALU.add,
+                )
             if ORD == 0 or (ORD == 2 and x_at.get(m - 1)):
                 terms(m)
             for n in []:

@@ -65,7 +65,7 @@ NPE = 1
 NPE_LATE = 1
 ORD = 1
 SHARE = 1
-BCV = list(range(0, 46, 4))
+BCV = []
 VNLAG = 1
 VNSTEP = 1
 R0FIRST = 2

@@ -40,7 +40,7 @@ XS = -5
 SHIFT_ON = "g"
 RB = 5
 LNB = 4
-OB = 4
+OB = 6
 VEXIT = 0
 VM_FROM = 48
 VTAKE = 0
@@ -54,11 +54,11 @@ LAST = 0
 CNUM = 1
 CDEN = 2
 CSP = 3
-XSTEP = 1.0
+XSTEP = 2.0
 CHAIN = []
-VNORM = [(3, 1)]
+VNORM = []
 VN0 = 32
-HEADS = (0, 2, 4, 8)
+HEADS = (0, 0, 4, 8)
 PIECES = ((3, 0, 4), (2, 4, 8), (1, 8, 12))
 PIECES2 = ((2, 0, 6), (1, 6, 12))
 NPE = 1
@@ -66,15 +66,24 @@ NPE_LATE = 1
 ORD = 1
 SHARE = 1
 BCV = []
+FIRST_PIECES = 2
+SPLIT_FROM = 47
+TAIL_PE = 46
+PAIR0 = 36
 VNLAG = 1
 VNSTEP = 1
 R0FIRST = 2
 BACKFIRST = 1
-NORM_AT = 0
+XB = 4
+QLAG = 2
+QPOS = 3
+RSTEP = 1.0
+S1 = []
+NORM_AT = -2
 VNRATE = 1
 GLN = []
 EV = 0
-NMLAG = 5
+NMLAG = 6
 FLOPS = 2 * BATCH * LAYERS * SEQ * D * D * OUTPUTS
 
 
@@ -102,6 +111,7 @@ def tile_dcadecoderblock_pa_t_kernel(
         code_pool = stack.enter_context(tc.tile_pool(name="codes", bufs=CHUNKS * LAYERS))
         ln_pool = stack.enter_context(tc.tile_pool(name="ln", bufs=LNB))
         relu_pool = stack.enter_context(tc.tile_pool(name="relu", bufs=LEAD + LT + RB))
+        extra_pool = stack.enter_context(tc.tile_pool(name="extra", bufs=XB))
         out_pool = stack.enter_context(tc.tile_pool(name="out", bufs=OB))
         prod_psum = stack.enter_context(tc.psum_pool(name="prod", bufs=PROD + TURN * SHARE))
         turn_psum = stack.enter_context(tc.psum_pool(name="turn", bufs=TURN))
@@ -126,7 +136,12 @@ def tile_dcadecoderblock_pa_t_kernel(
             if len(xs) == c:
                 xs.append(x_pool.tile([P, LAYERS, TILES, D], BF16, name="x"))
             for l in layers:
-                nc.sync.dma_start(out=xs[c][:, l], in_=token_view(layer_outputs[b, l, rows, :]))
+                pieces = FIRST_PIECES if (c, l) == (0, 0) else 1
+                step = TILES // pieces
+                for i in range(0, TILES, step):
+                    nc.sync.dma_start(
+                        out=xs[c][:, l, i : i + step], in_=token_view(layer_outputs[b, l, rows, :])[:, i : i + step]
+                    )
 
         xs = []
         load_x(0, range(LAYERS))
@@ -276,16 +291,23 @@ def tile_dcadecoderblock_pa_t_kernel(
                 rhs=codes[:].bitcast(FP8X4), rhs_scale=scales[:],
                 start=True, stop=True,
             )
-            if l == 0 and units.index((c, j, t)) not in CHAIN:
+            if l == 1 and units.index((c, j, t)) in S1:
+                extra = extra_pool.tile([P, CHUNK], F32, name="extra")
+                nc.scalar.activation(out=extra[:], in_=prod[:], func=ACT.Relu, bias=bias[:, t, j : j + 1], scale=1.0)
+                extras[(c, j, t)] = extra
+            elif l == 0 and units.index((c, j, t)) not in CHAIN:
                 relu_sums[(c, j, t)] = relu_pool.tile([P, CHUNK], F32, name="relu")
                 nc.scalar.activation(
                     out=relu_sums[(c, j, t)][:], in_=prod[:], func=ACT.Relu, bias=bias[:, t, j : j + 1], scale=1.0
                 )
             else:
-                nc.vector.scalar_tensor_tensor(
-                    out=relu_sums[(c, j, t)][:], in0=prod[:], scalar=neg_bias[:, t, j : j + 1],
-                    in1=relu_sums[(c, j, t)][:], op0=ALU.max, op1=ALU.add,
-                )
+                parts_of = 2 if l == LAYERS - 1 and units.index((c, j, t)) >= SPLIT_FROM else 1
+                for h in range(parts_of):
+                    cols = slice(h * CHUNK // parts_of, (h + 1) * CHUNK // parts_of)
+                    nc.vector.scalar_tensor_tensor(
+                        out=relu_sums[(c, j, t)][:, cols], in0=prod[:, cols], scalar=neg_bias[:, t, j : j + 1],
+                        in1=relu_sums[(c, j, t)][:, cols], op0=ALU.max, op1=ALU.add,
+                    )
 
         def sum_steps(c):
             layers = [l for l in range(LAYERS) if (c, l) not in VNORM]
@@ -311,7 +333,7 @@ def tile_dcadecoderblock_pa_t_kernel(
             else:
                 ln = ln_pool.tile([P, CHUNK], F32, name="ln")
                 norm_terms[(c, j, t)] = ln
-            shift_by = offset3 if n in CHAIN else offset
+            shift_by = offset3 if n in CHAIN else offset1 if n in S1 else offset
             if n in GLN:
                 nc.gpsimd.tensor_scalar(
                     out=ln[:], in0=flat_sums[(c, j)][:], scalar1=gain[:, t, j : j + 1], scalar2=shift_by[:, t, j : j + 1],
@@ -334,20 +356,32 @@ def tile_dcadecoderblock_pa_t_kernel(
             bank = (prod_psum if SHARE else turn_psum).tile([P, TILES, P], F32, name="back", tag="bank" if SHARE else "turn")
             for i in range(TILES):
                 tokens = slice(i * P, (i + 1) * P)
-                merged = i >= npe
-                nc.tensor.matmul(
-                    out=bank[:, i, :], lhsT=relu_sums[(c, j, t)][:, tokens], rhs=ident[:],
-                    is_transpose=True, start=True, stop=merged,
-                )
-                if not merged:
+                sources = [relu_sums[(c, j, t)]]
+                if (c, j, t) in extras:
+                    sources.append(extras[(c, j, t)])
+                if i < npe:
+                    sources.append(norm_terms[(c, j, t)])
+                for k, source in enumerate(sources):
                     nc.tensor.matmul(
-                        out=bank[:, i, :], lhsT=norm_terms[(c, j, t)][:, tokens], rhs=ident[:],
-                        is_transpose=True, start=False, stop=True,
+                        out=bank[:, i, :], lhsT=source[:, tokens], rhs=ident[:],
+                        is_transpose=True, start=k == 0, stop=k == len(sources) - 1,
                     )
             backs[(c, j, t)] = bank
 
         def take_back(c, j, t, on_vector):
             result = out_pool.tile([P, TILES, P], F32, name="result")
+            if units.index((c, j, t)) >= SPLIT_FROM:
+                b, rows = chunk_rows(c)
+                for h in range(2):
+                    tiles = slice(h * TILES // 2, (h + 1) * TILES // 2)
+                    if h:
+                        nc.vector.tensor_copy(out=result[:, tiles], in_=backs[(c, j, t)][:, tiles])
+                    else:
+                        nc.scalar.copy(out=result[:, tiles], in_=backs[(c, j, t)][:, tiles])
+                    nc.sync.dma_start(
+                        out=token_view(outs[t][b, rows, j * P : (j + 1) * P])[:, tiles], in_=result[:, tiles]
+                    )
+                return
             if on_vector:
                 nc.vector.tensor_copy(out=result[:], in_=backs[(c, j, t)][:])
             else:
@@ -365,6 +399,8 @@ def tile_dcadecoderblock_pa_t_kernel(
 
         offset3 = consts.tile([P, OUTPUTS, BLOCKS], F32)
         flat_sums = {}
+        extras = {}
+        offset1 = consts.tile([P, OUTPUTS, BLOCKS], F32)
         turned_rows = []
 
         def make_rows():
@@ -377,23 +413,28 @@ def tile_dcadecoderblock_pa_t_kernel(
             nc.vector.tensor_copy(
                 out=bias[:].rearrange("p t j -> p (t j)"), in_=turned_rows[0][:, 0 : OUTPUTS * BLOCKS]
             )
-            nc.vector.tensor_scalar(out=neg_bias[:], in0=bias[:], scalar1=-1.0, scalar2=None, op0=ALU.mult)
 
         def make_norm_rows():
             columns_ps = (prod_psum if SHARE else turn_psum).tile([P, P], F32, name="columns_ps", tag="bank" if SHARE else "turn")
             nc.tensor.transpose(columns_ps[:], norm_f32[:], ident[:])
             turned_rows.append(columns_ps)
 
-        def make_norm_columns():
-            nc.vector.tensor_copy(
-                out=columns[:].rearrange("p v t j -> p (v t j)"), in_=turned_rows[1][:, 0 : 2 * OUTPUTS * BLOCKS]
-            )
-            nc.vector.tensor_scalar(
-                out=offset[:], in0=columns[:, 1, :, :], scalar1=float(LAYERS), scalar2=None, op0=ALU.mult
-            )
+        def make_norm_columns(step):
+            if step == 0:
+                nc.vector.tensor_copy(
+                    out=columns[:].rearrange("p v t j -> p (v t j)"), in_=turned_rows[1][:, 0 : 2 * OUTPUTS * BLOCKS]
+                )
+                return
+            if step == 1:
+                nc.vector.tensor_scalar(
+                    out=offset[:], in0=columns[:, 1, :, :], scalar1=float(LAYERS), scalar2=None, op0=ALU.mult
+                )
+                return
             nc.vector.scalar_tensor_tensor(
                 out=offset[:], in0=bias[:], scalar=float(LAYERS - 1), in1=offset[:], op0=ALU.mult, op1=ALU.add
             )
+            if S1:
+                nc.vector.tensor_tensor(out=offset1[:], in0=offset[:], in1=bias[:], op=ALU.subtract)
             if CHAIN:
                 nc.vector.tensor_tensor(out=offset3[:], in0=offset[:], in1=bias[:], op=ALU.add)
 
@@ -418,26 +459,27 @@ def tile_dcadecoderblock_pa_t_kernel(
         head_units = [(0, j, t) for t in range(OUTPUTS) for j in range(BLOCKS)] + [units[n] for n in firsts[12:]]
         for i in range(3):
             statistics(0, 0, i)
-        make_rows()
         quantise(0, 0)
+        make_rows()
         statistics(0, 0, 3)
-        make_columns()
-        for i in range(TILES):
+        for i in range(TILES - 1):
             aggregate(0, 0, i)
+        make_columns()
+        aggregate(0, 0, 3)
         for l in range(1, LAYERS):
             first_relus(HEADS[l - 1], HEADS[l])
             deviation(0, l - 1)
-            statistics(0, l, 0)
-            quantise(0, l)
             inverse(0, l - 1)
             for i in range(TILES):
                 normalise(0, l - 1, i)
-            for i in range(1, TILES):
+            for i in range(TILES):
                 statistics(0, l, i)
+                if i == QPOS:
+                    quantise(0, l)
             for i in range(TILES):
                 aggregate(0, l, i)
         first_relus(HEADS[2], HEADS[3])
-        nc.vector.tensor_copy(out=norm_f32[:], in_=norm_rows[:])
+        nc.vector.tensor_scalar(out=neg_bias[:], in0=bias[:], scalar1=-1.0, scalar2=None, op0=ALU.mult)
 
         x_halves = [(c, l, half) for c in range(1, CHUNKS) for l in range(LAYERS) for half in range(HALVES)]
         x_tiles = [(c, l, i) for c in range(1, CHUNKS) for l in range(LAYERS) for i in range(TILES)]
@@ -453,13 +495,17 @@ def tile_dcadecoderblock_pa_t_kernel(
 
         catch = (CHUNKS - 1) * BLOCKS * OUTPUTS
 
-        def term_round(n):
+        def unit_round(n):
             if n in CHAIN:
                 return n - 1
             return n + LT if n < catch else max(n + LAST, catch + LT + ((n - catch) * CNUM) // CDEN)
 
+        def term_round(n):
+            return unit_round(n)
+
         def merge_round(n):
-            return max(term_round(n) + 1, n + 1) if n not in CHAIN else n
+            late = n >= PAIR0 and (n - PAIR0) % 2 == 0
+            return max(unit_round(n) + 1, term_round(n) + 1, n + 1 + late) if n not in CHAIN else n
 
         terms_at = {}
         merges_at = {}
@@ -468,14 +514,19 @@ def tile_dcadecoderblock_pa_t_kernel(
             terms_at.setdefault(term_round(n), []).append(n)
             merges_at.setdefault(merge_round(n), []).append(n)
             if n % OUTPUTS == 0:
-                pieces = PIECES if n < catch + CSP else PIECES2
+                pieces = PIECES if 0 < n < catch + CSP else PIECES2
                 for back, first, last in pieces:
                     sums_at.setdefault(term_round(n) - back, []).append((n, first, last))
         last_round = merge_round(len(units) - 1) + 2
+        for n in range(TAIL_PE, len(units)):
+            merges_at[merge_round(n)].remove(n)
+            merges_at.setdefault(merge_round(n) - 1, []).append(n)
 
         def npe_of(n):
             if n in CHAIN:
                 return 0
+            if n >= TAIL_PE:
+                return TILES
             if merge_round(n) >= VM_FROM:
                 return 0
             if NPE < 0:
@@ -490,8 +541,18 @@ def tile_dcadecoderblock_pa_t_kernel(
             x_at.setdefault(x_round(k), []).append(h)
         firsts_at = {}
         for k in range(HEADS[3], len(firsts)):
-            r = k - LEAD if k >= min(LEAD, 12) else -SHIFT + ((k - HEADS[3]) * (12 - LEAD + SHIFT)) // (12 - HEADS[3])
+            r = int((k - LEAD) * RSTEP) if k >= min(LEAD, 12) else -SHIFT + ((k - HEADS[3]) * (12 - LEAD + SHIFT)) // (12 - HEADS[3])
             firsts_at.setdefault(r, []).append(k)
+
+        adds_at = {}
+        for n in range(len(units)):
+            if n < PAIR0:
+                places = ((n, 0), (n, 1))
+            else:
+                pair = n - (n - PAIR0) % 2
+                places = ((pair, n - pair), (pair + 1, n - pair))
+            for l, place in zip((1, 2), places):
+                adds_at.setdefault(place, []).append((n, l))
 
         vn_at = {}
         for c, l in VNORM:
@@ -527,8 +588,8 @@ def tile_dcadecoderblock_pa_t_kernel(
                 multiply(*units[m], 0)
             if R0FIRST == 1:
                 r0s(m)
-            if unit_at(m):
-                multiply(*units[m], 1)
+            for n, l in adds_at.get((m, 0), []):
+                multiply(*units[n], l)
             if tile:
                 statistics(*tile)
             if R0FIRST == 2:
@@ -536,13 +597,17 @@ def tile_dcadecoderblock_pa_t_kernel(
             for n in merges_at.get(m, []):
                 if npe_of(n) < TILES and n not in CHAIN:
                     merge(*units[n], m >= VM_FROM, npe_of(n))
-            if unit_at(m):
-                multiply(*units[m], 2)
+            for n, l in adds_at.get((m, 1), []):
+                multiply(*units[n], l)
             if R0FIRST == 0:
                 r0s(m)
-            if m == NORM_AT:
-                make_norm_columns()
-            if tile:
+            if NORM_AT <= m < NORM_AT + 3:
+                make_norm_columns(m - NORM_AT)
+            if m == NORM_AT - 2:
+                nc.vector.tensor_copy(out=norm_f32[:], in_=norm_rows[:])
+            if m <= 0 and tile_at(m + SHIFT - 1):
+                aggregate(*tile_at(m + SHIFT - 1))
+            if tile and m >= 0:
                 aggregate(*tile)
             done = tile_at(m + SHIFT - 1)
             if done and done[2] == TILES - 1:
@@ -571,7 +636,7 @@ def tile_dcadecoderblock_pa_t_kernel(
                     flatten_sums(*units[n][0:2])
                 norm_term(*units[n])
             for k, h in enumerate(x_halves):
-                if h[2] == HALVES - 1 and x_round(k) + 2 == m:
+                if h[2] == HALVES - 1 and x_round(k) + QLAG == m:
                     quantise(*h[0:2])
             if m == NORM_AT - 1:
                 make_norm_rows()

from contextlib import ExitStack

import concourse.mybir as mybir
from concourse.masks import make_identity

F32 = mybir.dt.float32
BF16 = mybir.dt.bfloat16
I32 = mybir.dt.int32
U32 = mybir.dt.uint32
U8 = mybir.dt.uint8
FP8X4 = mybir.dt.float8_e4m3fn_x4
ALU = mybir.AluOpType
ACT = mybir.ActivationFunctionType

P = 128
BATCH, LAYERS, SEQ, D = 2, 3, 1024, 512
EPS = 1e-5
BLOCKS = D // P
CHUNK = 512
TILES = CHUNK // P
CHUNKS = BATCH * SEQ // CHUNK
HALF = CHUNK // 2
HALVES = CHUNK // HALF
OUTPUTS = 3
LAG = BLOCKS * OUTPUTS

SHIFT = 5
LT = 3
PARTS = 24
PE_EVERY = 3
QSHIFT = 0
ORDER = 1
PROD = 3
TURN = 3
SUMS = 2
LEAD = 12
SPREAD = 1
XR = 1
XS = -5
SHIFT_ON = "g"
RB = 5
LNB = 4
OB = 6
VEXIT = 0
VM_FROM = 48
VTAKE = 0
PE_UNTIL = 42
VSUM = []
QB = 6
RSQRT = 1
THIRD_ON_V = 0
NEG_ON_G = 0
LAST = 0
CNUM = 1
CDEN = 2
CSP = 3
XSTEP = 2.0
CHAIN = []
VNORM = []
VN0 = 32
HEADS = (0, 0, 4, 8)
PIECES = ((3, 0, 4), (2, 4, 8), (1, 8, 12))
PIECES2 = ((2, 0, 6), (1, 6, 12))
NPE = 1
NPE_LATE = 1
ORD = 1
SHARE = 1
BCV = []
FIRST_PIECES = 2
SPLIT_FROM = 47
TAIL_PE = 46
PAIR0 = 36
VNLAG = 1
VNSTEP = 1
R0FIRST = 2
BACKFIRST = 1
XB = 4
QLAG = 2
QPOS = 3
RSTEP = 1.0
S1 = []
NORM_AT = -2
VNRATE = 1
GLN = []
EV = 0
NMLAG = 6
FLOPS = 2 * BATCH * LAYERS * SEQ * D * D * OUTPUTS


def tile_dcadecoderblock_pa_t_kernel(
    tc,
    layer_outputs,
    q_words, q_scales, q_b, q_g, q_be,
    k_words, k_scales, k_b, k_g, k_be,
    v_words, v_scales, v_b, v_g, v_be,
    out_q, out_k, out_v,
):
    nc = tc.nc
    words_in = (q_words, k_words, v_words)
    scales_in = (q_scales, k_scales, v_scales)
    vectors_in = ((q_b, q_g, q_be), (k_b, k_g, k_be), (v_b, v_g, v_be))
    outs = (out_q, out_k, out_v)

    with ExitStack() as stack:
        stack.enter_context(tc.manual_schedule())
        consts = stack.enter_context(tc.tile_pool(name="consts", bufs=1))
        x_pool = stack.enter_context(tc.tile_pool(name="x", bufs=CHUNKS))
        small = stack.enter_context(tc.tile_pool(name="small", bufs=3))
        part_pool = stack.enter_context(tc.tile_pool(name="part", bufs=PARTS))
        quant = stack.enter_context(tc.tile_pool(name="quant", bufs=QB))
        code_pool = stack.enter_context(tc.tile_pool(name="codes", bufs=CHUNKS * LAYERS))
        ln_pool = stack.enter_context(tc.tile_pool(name="ln", bufs=LNB))
        relu_pool = stack.enter_context(tc.tile_pool(name="relu", bufs=LEAD + LT + RB))
        extra_pool = stack.enter_context(tc.tile_pool(name="extra", bufs=XB))
        out_pool = stack.enter_context(tc.tile_pool(name="out", bufs=OB))
        prod_psum = stack.enter_context(tc.psum_pool(name="prod", bufs=PROD + TURN * SHARE))
        turn_psum = stack.enter_context(tc.psum_pool(name="turn", bufs=TURN))
        sums_psum = stack.enter_context(tc.psum_pool(name="sums", bufs=SUMS))

        ident = consts.tile([P, P], F32)
        make_identity(nc, ident[:])
        eps = consts.tile([P, 1], F32)
        nc.vector.memset(eps[:], EPS)
        warm = consts.tile([P, 1], F32)
        nc.scalar.activation(out=warm[:], in_=eps[:], func=ACT.Abs_reciprocal_sqrt if RSQRT else ACT.Sqrt)

        def token_view(rows):
            return rows.rearrange("(p i) f -> p i f", i=TILES)

        def chunk_rows(c):
            per_batch = SEQ // CHUNK
            return c // per_batch, slice((c % per_batch) * CHUNK, (c % per_batch + 1) * CHUNK)

        def load_x(c, layers):
            b, rows = chunk_rows(c)
            if len(xs) == c:
                xs.append(x_pool.tile([P, LAYERS, TILES, D], BF16, name="x"))
            for l in layers:
                pieces = FIRST_PIECES if (c, l) == (0, 0) else 1
                step = TILES // pieces
                for i in range(0, TILES, step):
                    nc.sync.dma_start(
                        out=xs[c][:, l, i : i + step], in_=token_view(layer_outputs[b, l, rows, :])[:, i : i + step]
                    )

        xs = []
        load_x(0, range(LAYERS))
        bias_rows = consts.tile([P, P], BF16)
        norm_rows = consts.tile([P, P], BF16)
        nc.vector.memset(bias_rows[:], 0.0)

        def load_vectors(rows, first_vector, vectors):
            for v in vectors:
                for t in range(OUTPUTS):
                    first = BLOCKS * (OUTPUTS * (v - first_vector) + t)
                    nc.sync.dma_start(
                        out=rows[first : first + BLOCKS, :],
                        in_=vectors_in[t][v].rearrange("(j m) -> j m", m=P),
                    )

        load_vectors(bias_rows, 0, [0])

        w_codes = consts.tile([P, OUTPUTS, D], U32, align_bytes=64)
        w_scales = consts.tile([P, OUTPUTS, D], U8, align_bytes=64)
        nc.vector.memset(w_scales[:].rearrange("p t n -> p (t n)").bitcast(I32), 0)
        for t in range(OUTPUTS):
            for quadrant in range(4):
                nc.sync.dma_start(
                    out=w_scales[32 * quadrant : 32 * quadrant + 4, t, :].bitcast(I32),
                    in_=scales_in[t][0, 4 * quadrant : 4 * quadrant + 4, :].bitcast(I32),
                )
            nc.sync.dma_start(
                out=w_codes[:, t, :].bitcast(I32),
                in_=words_in[t][0].rearrange("p n t -> p (n t)").bitcast(I32),
            )

        nc.vector.memset(norm_rows[:], 0.0)
        load_x(1, range(LAYERS))
        load_vectors(norm_rows, 1, [1, 2])
        for c in range(2, CHUNKS):
            load_x(c, range(LAYERS))

        six = {}
        mean_var = {}
        totals = {}
        grouped = {}
        operands = {}
        turned_x = {}
        turned_sums = {}
        relu_sums = {}
        norm_terms = {}
        backs = {}

        def statistics(c, l, i):
            if (l, i) == (0, 0):
                six[c] = small.tile([P, LAYERS, TILES, 6], F32, name="six")
                mean_var[c] = small.tile([P, LAYERS, TILES, 2], F32, name="mean_var")
            nc.vector.bn_stats(out=six[c][:, l, i, :], in_=xs[c][:, l, i, :])

        def aggregate(c, l, i):
            nc.vector.bn_aggr(out=mean_var[c][:, l, i, :], in_=six[c][:, l, i, :])

        stds = {}
        rstds = {}
        shifts = {}
        negs = {}
        parts = {}

        def deviation(c, l):
            if l == 0:
                stds[c] = small.tile([P, LAYERS, TILES], F32, name="std")
                rstds[c] = small.tile([P, LAYERS, TILES], F32, name="rstd")
            if RSQRT:
                nc.scalar.activation(
                    out=rstds[c][:, l, :], in_=mean_var[c][:, l, :, 1], func=ACT.Abs_reciprocal_sqrt, bias=eps[:], scale=1.0
                )
            else:
                nc.scalar.activation(
                    out=stds[c][:, l, :], in_=mean_var[c][:, l, :, 1], func=ACT.Sqrt, bias=eps[:], scale=1.0
                )
            if SHIFT_ON != "v":
                if l == 0:
                    negs[c] = small.tile([P, LAYERS, TILES], F32, name="neg")
                if NEG_ON_G:
                    nc.gpsimd.tensor_scalar(
                        out=negs[c][:, l, :], in0=mean_var[c][:, l, :, 0], scalar1=-1.0, scalar2=0.0, op0=ALU.mult, op1=ALU.add
                    )
                else:
                    nc.scalar.activation(out=negs[c][:, l, :], in_=mean_var[c][:, l, :, 0], func=ACT.Copy, scale=-1.0)

        def inverse(c, l):
            if l == 0:
                shifts[c] = small.tile([P, LAYERS, TILES], F32, name="shift")
            if not RSQRT:
                nc.vector.reciprocal(out=rstds[c][:, l, :], in_=stds[c][:, l, :])
            if SHIFT_ON == "v":
                nc.vector.scalar_tensor_tensor(
                    out=shifts[c][:, l, :], in0=mean_var[c][:, l, :, 0], scalar=-1.0, in1=rstds[c][:, l, :],
                    op0=ALU.mult, op1=ALU.mult,
                )
            else:
                nc.gpsimd.tensor_tensor(out=shifts[c][:, l, :], in0=negs[c][:, l, :], in1=rstds[c][:, l, :], op=ALU.mult)

        def normalise(c, l, i):
            part = part_pool.tile([P, D], F32, name="part")
            nc.gpsimd.tensor_scalar(
                out=part[:], in0=xs[c][:, l, i, :],
                scalar1=rstds[c][:, l, i : i + 1], scalar2=shifts[c][:, l, i : i + 1],
                op0=ALU.mult, op1=ALU.add,
            )
            parts[(c, l, i)] = part

        def turn_x(c, l, half):
            bank = (prod_psum if SHARE else turn_psum).tile([P, 2, HALF], F32, name="turned_x", tag="bank" if SHARE else "turn")
            for i in range(HALF // P):
                x_words = xs[c][:, l, half * (HALF // P) + i, :].bitcast(F32)
                for u in range(2):
                    nc.tensor.transpose(bank[:, u, i * P : (i + 1) * P], x_words[:, u : D // 2 : 2], ident[:])
            turned_x[(c, l, half)] = bank

        def take_x(c, l, half, on_vector=False):
            if half == 0:
                grouped[(c, l)] = quant.tile([P, CHUNK, 4], BF16, name="grouped", align_bytes=64)
            words = grouped[(c, l)][:].rearrange("p r t -> p (r t)").bitcast(F32).rearrange("p (r u) -> p r u", u=2)
            if on_vector:
                nc.vector.tensor_copy(
                    out=words[:, half * HALF : (half + 1) * HALF, :],
                    in_=turned_x[(c, l, half)][:].rearrange("p u r -> p r u"),
                )
            else:
                nc.scalar.copy(
                    out=words[:, half * HALF : (half + 1) * HALF, :],
                    in_=turned_x[(c, l, half)][:].rearrange("p u r -> p r u"),
                )

        def quantise(c, l):
            codes = code_pool.tile([P, CHUNK], U32, name="codes", align_bytes=64)
            scales = code_pool.tile([P, CHUNK], U8, name="scales", align_bytes=64)
            nc.vector.quantize_mx(
                out=codes[:].bitcast(FP8X4), scales=scales[:], in_=grouped[(c, l)][:].rearrange("p r t -> p (r t)")
            )
            operands[(c, l)] = (codes, scales)

        def multiply(c, j, t, l):
            block = slice(j * P, (j + 1) * P)
            codes, scales = operands[(c, l)]
            prod = prod_psum.tile([P, CHUNK], F32, name="prod", tag="bank" if SHARE else "prod")
            nc.tensor.matmul_mx(
                out=prod[:],
                lhsT=w_codes[:, t, block].bitcast(FP8X4), lhsT_scale=w_scales[:, t, block],
                rhs=codes[:].bitcast(FP8X4), rhs_scale=scales[:],
                start=True, stop=True,
            )
            if l == 1 and units.index((c, j, t)) in S1:
                extra = extra_pool.tile([P, CHUNK], F32, name="extra")
                nc.scalar.activation(out=extra[:], in_=prod[:], func=ACT.Relu, bias=bias[:, t, j : j + 1], scale=1.0)
                extras[(c, j, t)] = extra
            elif l == 0 and units.index((c, j, t)) not in CHAIN:
                relu_sums[(c, j, t)] = relu_pool.tile([P, CHUNK], F32, name="relu")
                nc.scalar.activation(
                    out=relu_sums[(c, j, t)][:], in_=prod[:], func=ACT.Relu, bias=bias[:, t, j : j + 1], scale=1.0
                )
            else:
                parts_of = 2 if l == LAYERS - 1 and units.index((c, j, t)) >= SPLIT_FROM else 1
                for h in range(parts_of):
                    cols = slice(h * CHUNK // parts_of, (h + 1) * CHUNK // parts_of)
                    nc.vector.scalar_tensor_tensor(
                        out=relu_sums[(c, j, t)][:, cols], in0=prod[:, cols], scalar=neg_bias[:, t, j : j + 1],
                        in1=relu_sums[(c, j, t)][:, cols], op0=ALU.max, op1=ALU.add,
                    )

        def sum_steps(c):
            layers = [l for l in range(LAYERS) if (c, l) not in VNORM]
            return [(i, l, layers) for i in range(TILES) for l in layers]

        def turn_sums(c, j, first, last):
            if first == 0:
                turned_sums[(c, j)] = sums_psum.tile([P, CHUNK], F32, name="turned_sums")
            bank = turned_sums[(c, j)]
            steps = sum_steps(c)
            for i, l, layers in steps[len(steps) * first // 12 : len(steps) * last // 12]:
                if True:
                    nc.tensor.matmul(
                        out=bank[:, i * P : (i + 1) * P], lhsT=parts[(c, l, i)][:, j * P : (j + 1) * P], rhs=ident[:],
                        is_transpose=True, start=l == 0, stop=l == layers[-1],
                    )

        def norm_term(c, j, t):
            n = units.index((c, j, t))
            if n in CHAIN:
                ln = relu_pool.tile([P, CHUNK], F32, name="relu")
                relu_sums[(c, j, t)] = ln
            else:
                ln = ln_pool.tile([P, CHUNK], F32, name="ln")
                norm_terms[(c, j, t)] = ln
            shift_by = offset3 if n in CHAIN else offset1 if n in S1 else offset
            if n in GLN:
                nc.gpsimd.tensor_scalar(
                    out=ln[:], in0=flat_sums[(c, j)][:], scalar1=gain[:, t, j : j + 1], scalar2=shift_by[:, t, j : j + 1],
                    op0=ALU.mult, op1=ALU.add,
                )
            else:
                nc.scalar.activation(
                    out=ln[:], in_=turned_sums[(c, j)][:], func=ACT.Identity,
                    scale=gain[:, t, j : j + 1], bias=shift_by[:, t, j : j + 1],
                )

        def merge(c, j, t, on_vector, npe):
            engine = nc.vector if on_vector else nc.gpsimd
            cols = slice(npe * P, CHUNK)
            engine.tensor_tensor(
                out=relu_sums[(c, j, t)][:, cols], in0=relu_sums[(c, j, t)][:, cols], in1=norm_terms[(c, j, t)][:, cols], op=ALU.add
            )

        def turn_back(c, j, t, npe):
            bank = (prod_psum if SHARE else turn_psum).tile([P, TILES, P], F32, name="back", tag="bank" if SHARE else "turn")
            for i in range(TILES):
                tokens = slice(i * P, (i + 1) * P)
                sources = [relu_sums[(c, j, t)]]
                if (c, j, t) in extras:
                    sources.append(extras[(c, j, t)])
                if i < npe:
                    sources.append(norm_terms[(c, j, t)])
                for k, source in enumerate(sources):
                    nc.tensor.matmul(
                        out=bank[:, i, :], lhsT=source[:, tokens], rhs=ident[:],
                        is_transpose=True, start=k == 0, stop=k == len(sources) - 1,
                    )
            backs[(c, j, t)] = bank

        def take_back(c, j, t, on_vector):
            result = out_pool.tile([P, TILES, P], F32, name="result")
            if units.index((c, j, t)) >= SPLIT_FROM:
                b, rows = chunk_rows(c)
                for h in range(2):
                    tiles = slice(h * TILES // 2, (h + 1) * TILES // 2)
                    if h:
                        nc.vector.tensor_copy(out=result[:, tiles], in_=backs[(c, j, t)][:, tiles])
                    else:
                        nc.scalar.copy(out=result[:, tiles], in_=backs[(c, j, t)][:, tiles])
                    nc.sync.dma_start(
                        out=token_view(outs[t][b, rows, j * P : (j + 1) * P])[:, tiles], in_=result[:, tiles]
                    )
                return
            if on_vector:
                nc.vector.tensor_copy(out=result[:], in_=backs[(c, j, t)][:])
            else:
                nc.scalar.copy(out=result[:], in_=backs[(c, j, t)][:])
            b, rows = chunk_rows(c)
            nc.sync.dma_start(out=token_view(outs[t][b, rows, j * P : (j + 1) * P]), in_=result[:])

        rows_f32 = consts.tile([P, P], F32)
        norm_f32 = consts.tile([P, P], F32)
        bias = consts.tile([P, OUTPUTS, BLOCKS], F32)
        columns = consts.tile([P, 2, OUTPUTS, BLOCKS], F32)
        gain = columns[:, 0, :, :]
        neg_bias = consts.tile([P, OUTPUTS, BLOCKS], F32)
        offset = consts.tile([P, OUTPUTS, BLOCKS], F32)

        offset3 = consts.tile([P, OUTPUTS, BLOCKS], F32)
        flat_sums = {}
        extras = {}
        offset1 = consts.tile([P, OUTPUTS, BLOCKS], F32)
        turned_rows = []

        def make_rows():
            nc.vector.tensor_copy(out=rows_f32[:], in_=bias_rows[:])
            columns_ps = (prod_psum if SHARE else turn_psum).tile([P, P], F32, name="columns_ps", tag="bank" if SHARE else "turn")
            nc.tensor.transpose(columns_ps[:], rows_f32[:], ident[:])
            turned_rows.append(columns_ps)

        def make_columns():
            nc.vector.tensor_copy(
                out=bias[:].rearrange("p t j -> p (t j)"), in_=turned_rows[0][:, 0 : OUTPUTS * BLOCKS]
            )

        def make_norm_rows():
            columns_ps = (prod_psum if SHARE else turn_psum).tile([P, P], F32, name="columns_ps", tag="bank" if SHARE else "turn")
            nc.tensor.transpose(columns_ps[:], norm_f32[:], ident[:])
            turned_rows.append(columns_ps)

        def make_norm_columns(step):
            if step == 0:
                nc.vector.tensor_copy(
                    out=columns[:].rearrange("p v t j -> p (v t j)"), in_=turned_rows[1][:, 0 : 2 * OUTPUTS * BLOCKS]
                )
                return
            if step == 1:
                nc.vector.tensor_scalar(
                    out=offset[:], in0=columns[:, 1, :, :], scalar1=float(LAYERS), scalar2=None, op0=ALU.mult
                )
                return
            nc.vector.scalar_tensor_tensor(
                out=offset[:], in0=bias[:], scalar=float(LAYERS - 1), in1=offset[:], op0=ALU.mult, op1=ALU.add
            )
            if S1:
                nc.vector.tensor_tensor(out=offset1[:], in0=offset[:], in1=bias[:], op=ALU.subtract)
            if CHAIN:
                nc.vector.tensor_tensor(out=offset3[:], in0=offset[:], in1=bias[:], op=ALU.add)

        def flatten_sums(c, j):
            flat = ln_pool.tile([P, CHUNK], F32, name="flat")
            if EV:
                nc.vector.tensor_copy(out=flat[:], in_=turned_sums[(c, j)][:])
            else:
                nc.scalar.copy(out=flat[:], in_=turned_sums[(c, j)][:])
            flat_sums[(c, j)] = flat

        units = [(c, j, t) for c in range(CHUNKS) for j in range(BLOCKS) for t in range(OUTPUTS)]
        firsts = [n for n in range(len(units)) if n not in CHAIN]
        for l in range(LAYERS):
            for half in range(HALVES):
                turn_x(0, l, half)
                take_x(0, l, half)
        def first_relus(a, b):
            for k in range(a, b):
                multiply(*head_units[k], 0)

        head_units = [(0, j, t) for t in range(OUTPUTS) for j in range(BLOCKS)] + [units[n] for n in firsts[12:]]
        for i in range(3):
            statistics(0, 0, i)
        quantise(0, 0)
        make_rows()
        statistics(0, 0, 3)
        for i in range(TILES - 1):
            aggregate(0, 0, i)
        make_columns()
        aggregate(0, 0, 3)
        for l in range(1, LAYERS):
            first_relus(HEADS[l - 1], HEADS[l])
            deviation(0, l - 1)
            inverse(0, l - 1)
            for i in range(TILES):
                normalise(0, l - 1, i)
            for i in range(TILES):
                statistics(0, l, i)
                if i == QPOS:
                    quantise(0, l)
            for i in range(TILES):
                aggregate(0, l, i)
        first_relus(HEADS[2], HEADS[3])
        nc.vector.tensor_scalar(out=neg_bias[:], in0=bias[:], scalar1=-1.0, scalar2=None, op0=ALU.mult)

        x_halves = [(c, l, half) for c in range(1, CHUNKS) for l in range(LAYERS) for half in range(HALVES)]
        x_tiles = [(c, l, i) for c in range(1, CHUNKS) for l in range(LAYERS) for i in range(TILES)]

        def unit_at(n):
            return units[n] if 0 <= n < len(units) else None

        def on_tensor(n):
            return n % PE_EVERY == 0 and n + LT + 1 < min(VM_FROM, PE_UNTIL)

        def tile_at(k):
            return x_tiles[k] if 0 <= k < len(x_tiles) else None

        catch = (CHUNKS - 1) * BLOCKS * OUTPUTS

        def unit_round(n):
            if n in CHAIN:
                return n - 1
            return n + LT if n < catch else max(n + LAST, catch + LT + ((n - catch) * CNUM) // CDEN)

        def term_round(n):
            return unit_round(n)

        def merge_round(n):
            late = n >= PAIR0 and (n - PAIR0) % 2 == 0
            return max(unit_round(n) + 1, term_round(n) + 1, n + 1 + late) if n not in CHAIN else n

        terms_at = {}
        merges_at = {}
        sums_at = {}
        for n in range(len(units)):
            terms_at.setdefault(term_round(n), []).append(n)
            merges_at.setdefault(merge_round(n), []).append(n)
            if n % OUTPUTS == 0:
                pieces = PIECES if 0 < n < catch + CSP else PIECES2
                for back, first, last in pieces:
                    sums_at.setdefault(term_round(n) - back, []).append((n, first, last))
        last_round = merge_round(len(units) - 1) + 2
        for n in range(TAIL_PE, len(units)):
            merges_at[merge_round(n)].remove(n)
            merges_at.setdefault(merge_round(n) - 1, []).append(n)

        def npe_of(n):
            if n in CHAIN:
                return 0
            if n >= TAIL_PE:
                return TILES
            if merge_round(n) >= VM_FROM:
                return 0
            if NPE < 0:
                return TILES if n % PE_EVERY == 0 and merge_round(n) < PE_UNTIL else 0
            return NPE if merge_round(n) < PE_UNTIL else NPE_LATE

        def x_round(k):
            return XS + k if k < 6 else XS + 6 + int((k - 6) * XSTEP)

        x_at = {}
        for k, h in enumerate(x_halves):
            x_at.setdefault(x_round(k), []).append(h)
        firsts_at = {}
        for k in range(HEADS[3], len(firsts)):
            r = int((k - LEAD) * RSTEP) if k >= min(LEAD, 12) else -SHIFT + ((k - HEADS[3]) * (12 - LEAD + SHIFT)) // (12 - HEADS[3])
            firsts_at.setdefault(r, []).append(k)

        adds_at = {}
        for n in range(len(units)):
            if n < PAIR0:
                places = ((n, 0), (n, 1))
            else:
                pair = n - (n - PAIR0) % 2
                places = ((pair, n - pair), (pair + 1, n - pair))
            for l, place in zip((1, 2), places):
                adds_at.setdefault(place, []).append((n, l))

        vn_at = {}
        for c, l in VNORM:
            base = (12 * (c - 1) + 4 * l + 3) - SHIFT + NMLAG
            for i in range(TILES):
                vn_at.setdefault(base + VNLAG + (i * VNSTEP if l == 1 else i), []).append((c, l, i))
        def r0s(m):
            for k in firsts_at.get(m, []):
                multiply(*head_units[k], 0)

        def terms(m):
            for n in terms_at.get(m, []):
                if n % OUTPUTS == 0 and any(k in GLN for k in range(n, n + OUTPUTS)):
                    flatten_sums(*units[n][0:2])
                norm_term(*units[n])

        for m in range(-SHIFT, last_round + 1):
            tail = m >= len(units)
            tile = tile_at(m + SHIFT)
            for k, n in enumerate(merges_at.get(m - 2, [])):
                take_back(*units[n], on_vector=tail and (m + k) % 2 == 1 or m < len(units) and n in BCV)
            for h in x_at.get(m - 1, []):
                take_x(*h)
            if ORD == 1 or (ORD == 2 and not x_at.get(m - 1)):
                terms(m)
            if m == -SHIFT + 1:
                deviation(0, LAYERS - 1)
            if m == -SHIFT + 2:
                inverse(0, LAYERS - 1)
                for i in range(TILES):
                    normalise(0, LAYERS - 1, i)
            if m in CHAIN:
                multiply(*units[m], 0)
            if R0FIRST == 1:
                r0s(m)
            for n, l in adds_at.get((m, 0), []):
                multiply(*units[n], l)
            if tile:
                statistics(*tile)
            if R0FIRST == 2:
                r0s(m)
            for n in merges_at.get(m, []):
                if npe_of(n) < TILES and n not in CHAIN:
                    merge(*units[n], m >= VM_FROM, npe_of(n))
            for n, l in adds_at.get((m, 1), []):
                multiply(*units[n], l)
            if R0FIRST == 0:
                r0s(m)
            if NORM_AT <= m < NORM_AT + 3:
                make_norm_columns(m - NORM_AT)
            if m == NORM_AT - 2:
                nc.vector.tensor_copy(out=norm_f32[:], in_=norm_rows[:])
            if m <= 0 and tile_at(m + SHIFT - 1):
                aggregate(*tile_at(m + SHIFT - 1))
            if tile and m >= 0:
                aggregate(*tile)
            done = tile_at(m + SHIFT - 1)
            if done and done[2] == TILES - 1:
                deviation(*done[0:2])
            done = tile_at(m + SHIFT - 2)
            if done and done[2] == TILES - 1:
                inverse(*done[0:2])
            tn = tile_at(m + SHIFT - NMLAG)
            if tn and (tn[0], tn[1]) not in VNORM and not (tn[1] == 0 and (tn[0], 1) in VNORM):
                normalise(*tn)
            if tn and tn[2] == TILES - 1 and (tn[0], tn[1]) in VNORM and (tn[0], tn[1] + 1) not in VNORM:
                c3 = tn[0]
                for l3 in range(1, tn[1] + 1):
                    nc.gpsimd.tensor_tensor(out=shifts[c3][:, 0, :], in0=shifts[c3][:, 0, :], in1=shifts[c3][:, l3, :], op=ALU.add)
                for i3 in range(TILES):
                    normalise(c3, 0, i3)
            for c3, l3, i3 in vn_at.get(m, []):
                nc.vector.scalar_tensor_tensor(
                    out=parts[(c3, 0, i3)][:], in0=xs[c3][:, l3, i3, :], scalar=rstds[c3][:, l3, i3 : i3 + 1],
                    in1=parts[(c3, 0, i3)][:], op0=ALU.mult, op1=ALU.add,
                )
            if ORD == 0 or (ORD == 2 and x_at.get(m - 1)):
                terms(m)
            for n in []:
                if n % OUTPUTS == 0 and any(k in GLN for k in range(n, n + OUTPUTS)):
                    flatten_sums(*units[n][0:2])
                norm_term(*units[n])
            for k, h in enumerate(x_halves):
                if h[2] == HALVES - 1 and x_round(k) + QLAG == m:
                    quantise(*h[0:2])
            if m == NORM_AT - 1:
                make_norm_rows()
            if BACKFIRST == 0:
                for h in x_at.get(m, []):
                    turn_x(*h)
            for n in merges_at.get(m - 1, []):
                turn_back(*units[n], npe_of(n))
            for n, first, last in sums_at.get(m, []):
                turn_sums(*units[n][0:2], first, last)
            if BACKFIRST == 1:
                for h in x_at.get(m, []):
                    turn_x(*h)
